import numpy as np
import ml_dtypes


def mxq(x, axis, fmt="e4m3"):
    dtype, down = {"e4m3": (ml_dtypes.float8_e4m3fn, 7), "e5m2": (ml_dtypes.float8_e5m2, 14)}[fmt]
    v = np.moveaxis(np.asarray(x, np.float32).astype(ml_dtypes.bfloat16).astype(np.float64), axis, -1)
    blocks = v.reshape(v.shape[:-1] + (-1, 32))
    amax = np.abs(blocks).max(-1, keepdims=True)
    byte = np.maximum(np.where(amax > 0, np.frexp(amax)[1] - 1 + 127, 0) - down, 1)
    scale = np.exp2(byte - 127.0)
    codes = (blocks / scale).astype(np.float32).astype(dtype).astype(np.float64)
    return np.moveaxis((codes * scale).reshape(v.shape), -1, axis)


WIDE = False


def mx_kscale(k):
    if not WIDE:
        return np.ones(k)
    levels = np.array([10, -10, 5, -5, 0])
    a = np.random.permutation(np.resize(levels, k // 512 * 4)).reshape(k // 512, 4)
    idx = np.arange(k)
    return np.exp2(a[idx // 512, idx % 128 // 32])


BF16 = ml_dtypes.bfloat16


def bf(x):
    return np.asarray(x, np.float32).astype(BF16)


def f64(x):
    return np.asarray(x).astype(np.float64)


E2M1 = np.array([0.0, 0.5, 1.0, 1.5, 2.0, 3.0, 4.0, 6.0, -0.0, -0.5, -1.0, -1.5, -2.0, -3.0, -4.0, -6.0])


def pack_weight(w, fmt):
    k, n = w.shape
    w = f64(bf(w)).reshape(k // 32, 32, n)
    amax = np.abs(w).max(1)
    if fmt == "e4m3":
        byte = np.frexp(amax)[1] - 1 + 127 - 7
    else:
        mant, ex = np.frexp(amax / 6.0)
        byte = np.where(mant > 0.5, ex, ex - 1) + 127
    byte = np.clip(np.where(amax > 0, byte, 1), 1, 254)
    scaled = (w * np.exp2(127.0 - byte)[:, None, :]).reshape(k, n).astype(np.float32)
    by_word = np.ascontiguousarray(scaled.reshape(k // 512, 128, 4, n).transpose(0, 1, 3, 2))
    if fmt == "e4m3":
        words = by_word.astype(ml_dtypes.float8_e4m3fn).view(np.uint8)
    else:
        c = by_word.astype(ml_dtypes.float4_e2m1fn).view(np.uint8) & 0xF
        words = c[..., 0::2] | (c[..., 1::2] << 4)
    return np.ascontiguousarray(words), np.ascontiguousarray(byte.astype(np.uint8).reshape(k // 512, 16, n))


def unpack_weight(words, scales, fmt):
    g, p, n, _ = words.shape
    if fmt == "e4m3":
        vals = np.ascontiguousarray(words).view(ml_dtypes.float8_e4m3fn).astype(np.float64)
    else:
        nib = np.empty((g, p, n, 4), np.uint8)
        nib[..., 0::2] = words & 0xF
        nib[..., 1::2] = words >> 4
        vals = E2M1[nib]
    vals = vals * np.repeat(np.exp2(scales.astype(np.float64) - 127.0), 8, axis=1)[..., None]
    return vals.transpose(0, 1, 3, 2).reshape(g * 512, n)


B, T, D, H, HK, HV = 4, 256, 512, 4, 128, 2048
VD = H * HV
EPS = 1e-5
FMT = "e4m3"


def rmsnorm(v, w):
    var = np.mean(np.square(v), axis=-1, keepdims=True)
    return v * (1.0 / np.sqrt(var + EPS)) * w


def sigmoid(v):
    return 1.0 / (1.0 + np.exp(-v))


def setup_inputs():
    s = mx_kscale(D)
    th = mx_kscale(VD)[:HV]
    t = np.tile(th, H)
    g = np.random.standard_normal((B, T, H, HK))
    hidden_states = bf(np.random.standard_normal((B, T, D)))
    norm_w = bf((1.0 + 0.1 * np.random.standard_normal(D)) * s)
    gate_w = np.random.standard_normal((D, D)) / np.sqrt(D) / s[None, :]
    gate_w_words, gate_w_scales = pack_weight(np.ascontiguousarray(gate_w.T), FMT)
    q_hat = bf(g / np.sqrt(np.sum(np.square(g), axis=-1, keepdims=True)))
    recurrent_state = bf(np.random.standard_normal((B, H, HK, HV)))
    v_norm_w = bf((1.0 + 0.1 * np.random.standard_normal(HV)) * th)
    o_w = np.random.standard_normal((D, VD)) / np.sqrt(VD) / t[None, :]
    o_w_words, o_w_scales = pack_weight(np.ascontiguousarray(o_w.T), FMT)
    return {"hidden_states": hidden_states,
            "norm_w": norm_w,
            "gate_w_words": gate_w_words,
            "gate_w_scales": gate_w_scales,
            "q_hat": q_hat,
            "recurrent_state": recurrent_state,
            "v_norm_w": v_norm_w,
            "o_w_words": o_w_words,
            "o_w_scales": o_w_scales}


def reference(hidden_states, norm_w, gate_w_words, gate_w_scales, q_hat, recurrent_state, v_norm_w, o_w_words, o_w_scales):
    x = rmsnorm(f64(hidden_states), f64(norm_w)).reshape(B * T, D)
    o = f64(q_hat).transpose(0, 2, 1, 3) @ f64(recurrent_state)
    o = o.transpose(0, 2, 1, 3)
    o = rmsnorm(o, f64(v_norm_w)).reshape(B * T, VD)
    o = mxq(o, 1, "e4m3") @ unpack_weight(o_w_words, o_w_scales, FMT)
    gate = sigmoid(mxq(x, 1, "e4m3") @ unpack_weight(gate_w_words, gate_w_scales, FMT))
    return (gate * o).reshape(B, T, D)

@@ -1,0 +1,344 @@
+from contextlib import ExitStack
+
+import concourse.mybir as mybir
+from concourse.masks import make_identity
+
+F32 = mybir.dt.float32
+BF16 = mybir.dt.bfloat16
+I32 = mybir.dt.int32
+U32 = mybir.dt.uint32
+U8 = mybir.dt.uint8
+FP8X4 = mybir.dt.float8_e4m3fn_x4
+ACT = mybir.ActivationFunctionType
+ALU = mybir.AluOpType
+AXIS = mybir.AxisListType
+
+P = 128
+BATCH = 4
+SEQ = 256
+D_MODEL = 512
+HEADS = 4
+HEAD_V = 2048
+TOKEN_TILES = BATCH * SEQ // P
+TILES_PER_BATCH = SEQ // P
+BANK = 512
+BANKS = HEAD_V // BANK
+UNITS = TOKEN_TILES * HEADS
+READ_BANKS = 5
+EPS = 1e-5
+FLOPS = 2 * (1024 * 8192 * 512 + 1024 * 512 * 512 + 16 * 256 * 128 * 2048)
+
+
+def tile_glamemoryreader_pb_k_kernel(
+    tc,
+    hidden_states,
+    norm_w,
+    gate_w_words,
+    gate_w_scales,
+    q_hat,
+    recurrent_state,
+    v_norm_w,
+    o_w_words,
+    o_w_scales,
+    out,
+):
+    nc = tc.nc
+    with ExitStack() as ctx:
+        keep = ctx.enter_context(tc.tile_pool(name="keep", bufs=1))
+        work = ctx.enter_context(tc.tile_pool(name="work", bufs=3))
+        psum = ctx.enter_context(tc.psum_pool(name="psum", bufs=1))
+        ctx.enter_context(tc.manual_schedule())
+
+        ident_f32 = keep.tile([P, P], F32)
+        make_identity(nc, ident_f32[:])
+        ident_bf16 = keep.tile([P, P], BF16)
+        make_identity(nc, ident_bf16[:])
+        eps_sb = keep.tile([P, 1], F32)
+        nc.vector.memset(eps_sb[:], EPS)
+        gw_planes = keep.tile([P, D_MODEL], U8, align_bytes=64)
+        nc.vector.memset(gw_planes[:].bitcast(I32), 0)
+        ow_planes = keep.tile([P, HEADS * BANKS, D_MODEL], U8, align_bytes=64)
+        nc.vector.memset(ow_planes[:].bitcast(I32), 0)
+        sums = keep.tile([P, UNITS, 8], F32)
+        nc.vector.memset(sums[:], EPS)
+
+        x_sb = keep.tile([P, TOKEN_TILES, D_MODEL], BF16)
+        x_dram = hidden_states.rearrange("b (i p) d -> p (b i) d", p=P)
+        for half in range(2):
+            nc.sync.dma_start(out=x_sb[:, 4 * half : 4 * half + 4, :], in_=x_dram[:, 4 * half : 4 * half + 4, :])
+        nw_b = keep.tile([P, D_MODEL], BF16)
+        nc.sync.dma_start(out=nw_b[:], in_=norm_w.partition_broadcast(P))
+        gw_words = keep.tile([P, D_MODEL], U32, align_bytes=64)
+        nc.sync.dma_start(
+            out=gw_words[:].bitcast(I32),
+            in_=gate_w_words[0].rearrange("p n t -> p (n t)").bitcast(I32),
+        )
+        for r in range(4):
+            nc.sync.dma_start(out=gw_planes[r:P:32, :].bitcast(I32), in_=gate_w_scales[0, r:16:4, :].bitcast(I32))
+        q_sb = keep.tile([P, TOKEN_TILES, HEADS * P], BF16)
+        nc.sync.dma_start(out=q_sb[:], in_=q_hat.rearrange("b (i p) h k -> p (b i) (h k)", p=P))
+        state = [keep.tile([P, HEAD_V], BF16, name="state_%d" % bh) for bh in range(BATCH * HEADS)]
+        ow_words = [
+            keep.tile([P, BANKS, D_MODEL], U32, name="ow_words_%d" % h, align_bytes=64) for h in range(HEADS)
+        ]
+        vw_raw = keep.tile([P, HEAD_V], BF16)
+        nc.sync.dma_start(out=state[0][:], in_=recurrent_state[0, 0])
+        nc.sync.dma_start(out=vw_raw[:], in_=v_norm_w.partition_broadcast(P))
+        for r in range(4):
+            nc.sync.dma_start(
+                out=ow_planes[r:P:32, :, :].bitcast(I32),
+                in_=o_w_scales[:, r:16:4, :].rearrange("g c n -> c g n").bitcast(I32),
+            )
+        for h in range(HEADS):
+            if h > 0:
+                nc.sync.dma_start(out=state[h][:], in_=recurrent_state[0, h])
+            nc.sync.dma_start(
+                out=ow_words[h][:].bitcast(I32),
+                in_=o_w_words[BANKS * h : BANKS * (h + 1)].rearrange("g p n t -> p g (n t)").bitcast(I32),
+            )
+        for b in range(1, BATCH):
+            for h in range(HEADS):
+                nc.sync.dma_start(out=state[HEADS * b + h][:], in_=recurrent_state[b, h])
+
+        x_ms = keep.tile([P, TOKEN_TILES], F32)
+        x_std = keep.tile([P, TOKEN_TILES], F32)
+        x_rstd = keep.tile([P, TOKEN_TILES], F32)
+        xn = keep.tile([P, TOKEN_TILES, D_MODEL], BF16)
+        xg = keep.tile([P, TOKEN_TILES, P, 4], BF16, align_bytes=64)
+        x_codes = keep.tile([P, TOKEN_TILES, P], U32, align_bytes=64)
+        x_scales = keep.tile([P, TOKEN_TILES, P], U8, align_bytes=64)
+        gate_sb = keep.tile([P, TOKEN_TILES, D_MODEL], F32)
+        for half in range(2):
+            four = slice(4 * half, 4 * half + 4)
+            for i in range(4 * half, 4 * half + 4):
+                sq = work.tile([P, BANK], BF16, tag="sq", bufs=4)
+                nc.scalar.activation(
+                    out=sq[:], in_=x_sb[:, i, :], func=ACT.Square, scale=D_MODEL**-0.5, accum_out=x_ms[:, i : i + 1]
+                )
+            nc.scalar.activation(out=x_std[:, four], in_=x_ms[:, four], func=ACT.Sqrt, bias=eps_sb[:, 0:1])
+        x_turned = []
+        for half in range(2):
+            four = slice(4 * half, 4 * half + 4)
+            nc.vector.reciprocal(out=x_rstd[:, four], in_=x_std[:, four])
+            for i in range(4 * half, 4 * half + 4):
+                nc.vector.scalar_tensor_tensor(
+                    out=xn[:, i, :],
+                    in0=x_sb[:, i, :],
+                    scalar=x_rstd[:, i : i + 1],
+                    in1=nw_b[:],
+                    op0=ALU.mult,
+                    op1=ALU.mult,
+                )
+            for pair in range(2 * half, 2 * half + 2):
+                xt = psum.tile([P, 4, P], F32, tag="read", bufs=READ_BANKS)
+                for j in range(2):
+                    for u in range(2):
+                        nc.tensor.transpose(
+                            out=xt[:, 2 * j + u, :],
+                            in_=xn[:, 2 * pair + j, :].bitcast(F32)[:, u : D_MODEL // 2 : 2],
+                            identity=ident_f32[:],
+                        )
+                x_turned.append(xt)
+        for half in range(2):
+            for pair in range(2 * half, 2 * half + 2):
+                copy = nc.scalar.copy if half == 0 else nc.vector.tensor_copy
+                copy(
+                    out=xg[:, 2 * pair : 2 * pair + 2, :, :].bitcast(F32),
+                    in_=x_turned[pair][:].rearrange("p (i u) t -> p i t u", u=2),
+                )
+            four = slice(4 * half, 4 * half + 4)
+            nc.vector.quantize_mx(
+                out=x_codes[:, four, :].rearrange("p i t -> p (i t)").bitcast(FP8X4),
+                scales=x_scales[:, four, :].rearrange("p i t -> p (i t)"),
+                in_=xg[:, four, :, :].rearrange("p i t w -> p (i t w)"),
+            )
+        for i in range(TOKEN_TILES):
+            g_acc = psum.tile([P, BANK], F32, tag="read", bufs=READ_BANKS)
+            nc.tensor.matmul_mx(
+                out=g_acc[:],
+                lhsT=x_codes[:, i, :].bitcast(FP8X4),
+                lhsT_scale=x_scales[:, i, :],
+                rhs=gw_words[:].bitcast(FP8X4),
+                rhs_scale=gw_planes[:],
+                start=True,
+                stop=True,
+            )
+            nc.scalar.activation(out=gate_sb[:, i, :], in_=g_acc[:], func=ACT.Sigmoid)
+
+        q_t = keep.tile([P, UNITS, P], BF16)
+        for m in range(UNITS // 8):
+            qt_ps = psum.tile([P, 8, P], BF16, tag="turn", bufs=2)
+            for j in range(8):
+                nc.tensor.transpose(
+                    out=qt_ps[:, j, :],
+                    in_=q_sb[:, 2 * m + j // HEADS, P * (j % HEADS) : P * (j % HEADS + 1)],
+                    identity=ident_bf16[:],
+                )
+            nc.vector.tensor_copy(out=q_t[:, 8 * m : 8 * m + 8, :], in_=qt_ps[:])
+
+        w_sorted = keep.tile([P, HEAD_V], BF16)
+        nc.vector.tensor_copy(
+            out=w_sorted[:].bitcast(F32).rearrange("p (c u q) -> p c u q", c=BANKS, u=2),
+            in_=vw_raw[:].bitcast(F32).rearrange("p (c q u) -> p c u q", c=BANKS, u=2),
+        )
+
+        out_tiles = out.rearrange("b (i p) d -> (b i) p d", p=P)
+        r_banks = {}
+        biases = {}
+        stds = {}
+        rstds = {}
+        normed = {}
+        turned = {}
+        groups = {}
+        codes = {}
+        scales = {}
+        accs = {}
+
+        def exists(u):
+            return 0 <= u < UNITS
+
+        def read(u, c):
+            if not exists(u):
+                return
+            r_bank = psum.tile([P, BANK], F32, tag="read", bufs=READ_BANKS)
+            bh = HEADS * (u // HEADS // TILES_PER_BATCH) + u % HEADS
+            nc.tensor.matmul(
+                out=r_bank[:].rearrange("t (u p e) -> t p u e", u=2, e=2),
+                lhsT=q_t[:, u, :],
+                rhs=state[bh][:, BANK * c : BANK * (c + 1)].rearrange("k (p u e) -> k p u e", u=2, e=2),
+                start=True,
+                stop=True,
+            )
+            r_banks[(u, c)] = r_bank
+
+        def square(u, c):
+            if not exists(u):
+                return
+            sq = work.tile([P, BANK], BF16, tag="sq", bufs=4)
+            nc.scalar.activation(
+                out=sq[:],
+                in_=r_banks[(u, c)][:],
+                func=ACT.Square,
+                scale=HEAD_V**-0.5,
+                accum_out=sums[:, u, c + 1 : c + 2],
+            )
+
+        def partial(u):
+            if not exists(u):
+                return
+            bias = work.tile([P, 1], F32, tag="bias", bufs=4)
+            nc.vector.tensor_reduce(out=bias[:], in_=sums[:, u, 0:BANKS], axis=AXIS.X, op=ALU.add)
+            biases[u] = bias
+
+        def root(u):
+            if not exists(u):
+                return
+            std = work.tile([P, 1], F32, tag="std", bufs=4)
+            nc.scalar.activation(
+                out=std[:], in_=sums[:, u, BANKS : BANKS + 1], func=ACT.Sqrt, bias=biases[u][:, 0:1]
+            )
+            stds[u] = std
+
+        def invert(u):
+            if not exists(u):
+                return
+            rstd = work.tile([P, 1], F32, tag="rstd", bufs=4)
+            nc.vector.reciprocal(out=rstd[:], in_=stds[u][:])
+            rstds[u] = rstd
+
+        def normalise(u, c):
+            if not exists(u):
+                return
+            if c == 0:
+                rn = work.tile([P, HEAD_V], BF16, tag="rn")
+                normed[u] = rn
+            cols = slice(BANK * c, BANK * (c + 1))
+            nc.vector.scalar_tensor_tensor(
+                out=normed[u][:, cols],
+                in0=r_banks[(u, c)][:],
+                scalar=rstds[u][:, 0:1],
+                in1=w_sorted[:, cols],
+                op0=ALU.mult,
+                op1=ALU.mult,
+            )
+
+        def transpose(u):
+            if not exists(u):
+                return
+            words = normed[u][:].bitcast(F32)
+            for m in range(2):
+                rt = psum.tile([P, 4, P], F32, tag="turn", bufs=2)
+                for j in range(4):
+                    nc.tensor.transpose(
+                        out=rt[:, j, :], in_=words[:, P * (4 * m + j) : P * (4 * m + j + 1)], identity=ident_f32[:]
+                    )
+                turned[(u, m)] = rt
+
+        def regroup(u, m):
+            if not exists(u):
+                return
+            if m == 0:
+                grouped = work.tile([P, BANKS, P, 4], BF16, tag="grouped", align_bytes=64)
+                groups[u] = grouped
+            copy = nc.scalar.copy if m == 0 else nc.vector.tensor_copy
+            copy(
+                out=groups[u][:, 2 * m : 2 * m + 2, :, :].bitcast(F32),
+                in_=turned[(u, m)][:].rearrange("p (c u) t -> p c t u", u=2),
+            )
+
+        def quantise(u):
+            if not exists(u):
+                return
+            code = work.tile([P, BANKS, P], U32, tag="code", align_bytes=64)
+            scale = work.tile([P, BANKS, P], U8, tag="scale", align_bytes=64)
+            nc.vector.quantize_mx(
+                out=code[:].rearrange("p c t -> p (c t)").bitcast(FP8X4),
+                scales=scale[:].rearrange("p c t -> p (c t)"),
+                in_=groups[u][:].rearrange("p c t w -> p (c t w)"),
+            )
+            codes[u] = code
+            scales[u] = scale
+
+        def project(u, c):
+            if not exists(u):
+                return
+            h = u % HEADS
+            if h == 0 and c == 0:
+                acc = psum.tile([P, BANK], F32, tag="acc", bufs=1)
+                accs[u // HEADS] = acc
+            nc.tensor.matmul_mx(
+                out=accs[u // HEADS][:],
+                lhsT=codes[u][:, c, :].bitcast(FP8X4),
+                lhsT_scale=scales[u][:, c, :],
+                rhs=ow_words[h][:, c, :].bitcast(FP8X4),
+                rhs_scale=ow_planes[:, BANKS * h + c, :],
+                start=(h == 0 and c == 0),
+                stop=(h == HEADS - 1 and c == BANKS - 1),
+            )
+
+        def finish(u):
+            if not exists(u) or u % HEADS != HEADS - 1:
+                return
+            i = u // HEADS
+            o_sb = work.tile([P, D_MODEL], F32, tag="o_sb", bufs=2)
+            nc.vector.tensor_tensor(out=o_sb[:], in0=accs[i][:], in1=gate_sb[:, i, :], op=ALU.mult)
+            nc.sync.dma_start(out=out_tiles[i], in_=o_sb[:])
+
+        for u in range(-2, UNITS + 2):
+            regroup(u - 1, 0)
+            invert(u)
+            for c in range(BANKS - 1):
+                normalise(u, c)
+                read(u + 1, c + 1)
+                project(u - 2, c + 1)
+                square(u + 1, c + 1)
+            normalise(u, BANKS - 1)
+            read(u + 2, 0)
+            regroup(u - 1, 1)
+            partial(u + 1)
+            root(u + 1)
+            square(u + 2, 0)
+            transpose(u)
+            finish(u - 2)
+            quantise(u - 1)
+            project(u - 1, 0)

@@ -24,7 +24,7 @@ TILES_PER_BATCH = SEQ // P
 BANK = 512
 BANKS = HEAD_V // BANK
 UNITS = TOKEN_TILES * HEADS
-READ_BANKS = 5
+READ_BANKS = 4
 EPS = 1e-5
 FLOPS = 2 * (1024 * 8192 * 512 + 1024 * 512 * 512 + 16 * 256 * 128 * 2048)
 
@@ -45,7 +45,6 @@ def tile_glamemoryreader_pb_k_kernel(
     nc = tc.nc
     with ExitStack() as ctx:
         keep = ctx.enter_context(tc.tile_pool(name="keep", bufs=1))
-        work = ctx.enter_context(tc.tile_pool(name="work", bufs=3))
         psum = ctx.enter_context(tc.psum_pool(name="psum", bufs=1))
         ctx.enter_context(tc.manual_schedule())
 
@@ -62,131 +61,142 @@ def tile_glamemoryreader_pb_k_kernel(
         sums = keep.tile([P, UNITS, 8], F32)
         nc.vector.memset(sums[:], EPS)
 
-        x_sb = keep.tile([P, TOKEN_TILES, D_MODEL], BF16)
-        x_dram = hidden_states.rearrange("b (i p) d -> p (b i) d", p=P)
-        for half in range(2):
-            nc.sync.dma_start(out=x_sb[:, 4 * half : 4 * half + 4, :], in_=x_dram[:, 4 * half : 4 * half + 4, :])
-        nw_b = keep.tile([P, D_MODEL], BF16)
-        nc.sync.dma_start(out=nw_b[:], in_=norm_w.partition_broadcast(P))
-        gw_words = keep.tile([P, D_MODEL], U32, align_bytes=64)
-        nc.sync.dma_start(
-            out=gw_words[:].bitcast(I32),
-            in_=gate_w_words[0].rearrange("p n t -> p (n t)").bitcast(I32),
-        )
-        for r in range(4):
-            nc.sync.dma_start(out=gw_planes[r:P:32, :].bitcast(I32), in_=gate_w_scales[0, r:16:4, :].bitcast(I32))
-        q_sb = keep.tile([P, TOKEN_TILES, HEADS * P], BF16)
-        nc.sync.dma_start(out=q_sb[:], in_=q_hat.rearrange("b (i p) h k -> p (b i) (h k)", p=P))
+        gate_sb = keep.tile([P, TOKEN_TILES, D_MODEL], F32)
+        q_t = keep.tile([P, UNITS, P], BF16)
+        w_sorted = keep.tile([P, HEAD_V], BF16)
         state = [keep.tile([P, HEAD_V], BF16, name="state_%d" % bh) for bh in range(BATCH * HEADS)]
         ow_words = [
             keep.tile([P, BANKS, D_MODEL], U32, name="ow_words_%d" % h, align_bytes=64) for h in range(HEADS)
         ]
-        vw_raw = keep.tile([P, HEAD_V], BF16)
-        nc.sync.dma_start(out=state[0][:], in_=recurrent_state[0, 0])
-        nc.sync.dma_start(out=vw_raw[:], in_=v_norm_w.partition_broadcast(P))
-        for r in range(4):
+
+        with tc.tile_pool(name="front", bufs=1) as front:
+            x_sb = front.tile([P, TOKEN_TILES, D_MODEL], BF16)
+            x_dram = hidden_states.rearrange("b (i p) d -> p (b i) d", p=P)
+            for half in range(2):
+                four = slice(4 * half, 4 * half + 4)
+                nc.sync.dma_start(out=x_sb[:, four, :], in_=x_dram[:, four, :])
+            nw_b = front.tile([P, D_MODEL], BF16)
+            nc.sync.dma_start(out=nw_b[:], in_=norm_w.partition_broadcast(P))
+            gw_words = front.tile([P, D_MODEL], U32, align_bytes=64)
             nc.sync.dma_start(
-                out=ow_planes[r:P:32, :, :].bitcast(I32),
-                in_=o_w_scales[:, r:16:4, :].rearrange("g c n -> c g n").bitcast(I32),
+                out=gw_words[:].bitcast(I32),
+                in_=gate_w_words[0].rearrange("p n t -> p (n t)").bitcast(I32),
             )
-        for h in range(HEADS):
-            if h > 0:
-                nc.sync.dma_start(out=state[h][:], in_=recurrent_state[0, h])
-            nc.sync.dma_start(
-                out=ow_words[h][:].bitcast(I32),
-                in_=o_w_words[BANKS * h : BANKS * (h + 1)].rearrange("g p n t -> p g (n t)").bitcast(I32),
-            )
-        for b in range(1, BATCH):
+            for r in range(4):
+                nc.sync.dma_start(
+                    out=gw_planes[r:P:32, :].bitcast(I32), in_=gate_w_scales[0, r:16:4, :].bitcast(I32)
+                )
+            q_sb = front.tile([P, TOKEN_TILES, HEADS * P], BF16)
+            nc.sync.dma_start(out=q_sb[:], in_=q_hat.rearrange("b (i p) h k -> p (b i) (h k)", p=P))
+            vw_raw = front.tile([P, HEAD_V], BF16)
+            nc.sync.dma_start(out=state[0][:], in_=recurrent_state[0, 0])
+            nc.sync.dma_start(out=vw_raw[:], in_=v_norm_w.partition_broadcast(P))
+            for r in range(4):
+                nc.sync.dma_start(
+                    out=ow_planes[r:P:32, :, :].bitcast(I32),
+                    in_=o_w_scales[:, r:16:4, :].rearrange("g c n -> c g n").bitcast(I32),
+                )
             for h in range(HEADS):
-                nc.sync.dma_start(out=state[HEADS * b + h][:], in_=recurrent_state[b, h])
+                if h > 0:
+                    nc.sync.dma_start(out=state[h][:], in_=recurrent_state[0, h])
+                nc.sync.dma_start(
+                    out=ow_words[h][:].bitcast(I32),
+                    in_=o_w_words[BANKS * h : BANKS * (h + 1)].rearrange("g p n t -> p g (n t)").bitcast(I32),
+                )
+            for b in range(1, BATCH):
+                for h in range(HEADS):
+                    nc.sync.dma_start(out=state[HEADS * b + h][:], in_=recurrent_state[b, h])
 
-        x_ms = keep.tile([P, TOKEN_TILES], F32)
-        x_std = keep.tile([P, TOKEN_TILES], F32)
-        x_rstd = keep.tile([P, TOKEN_TILES], F32)
-        xn = keep.tile([P, TOKEN_TILES, D_MODEL], BF16)
-        xg = keep.tile([P, TOKEN_TILES, P, 4], BF16, align_bytes=64)
-        x_codes = keep.tile([P, TOKEN_TILES, P], U32, align_bytes=64)
-        x_scales = keep.tile([P, TOKEN_TILES, P], U8, align_bytes=64)
-        gate_sb = keep.tile([P, TOKEN_TILES, D_MODEL], F32)
-        for half in range(2):
-            four = slice(4 * half, 4 * half + 4)
-            for i in range(4 * half, 4 * half + 4):
-                sq = work.tile([P, BANK], BF16, tag="sq", bufs=4)
-                nc.scalar.activation(
-                    out=sq[:], in_=x_sb[:, i, :], func=ACT.Square, scale=D_MODEL**-0.5, accum_out=x_ms[:, i : i + 1]
+            x_ms = front.tile([P, TOKEN_TILES], F32)
+            x_std = front.tile([P, TOKEN_TILES], F32)
+            x_rstd = front.tile([P, TOKEN_TILES], F32)
+            xn = front.tile([P, TOKEN_TILES, D_MODEL], BF16)
+            xg = front.tile([P, TOKEN_TILES, P, 4], BF16, align_bytes=64)
+            x_codes = front.tile([P, TOKEN_TILES, P], U32, align_bytes=64)
+            x_scales = front.tile([P, TOKEN_TILES, P], U8, align_bytes=64)
+            for half in range(2):
+                four = slice(4 * half, 4 * half + 4)
+                for i in range(4 * half, 4 * half + 4):
+                    x_sq = front.tile([P, BANK], BF16, tag="x_sq", bufs=4)
+                    nc.scalar.activation(
+                        out=x_sq[:],
+                        in_=x_sb[:, i, :],
+                        func=ACT.Square,
+                        scale=D_MODEL**-0.5,
+                        accum_out=x_ms[:, i : i + 1],
+                    )
+                nc.scalar.activation(out=x_std[:, four], in_=x_ms[:, four], func=ACT.Sqrt, bias=eps_sb[:, 0:1])
+            x_turned = []
+            for half in range(2):
+                four = slice(4 * half, 4 * half + 4)
+                nc.vector.reciprocal(out=x_rstd[:, four], in_=x_std[:, four])
+                for i in range(4 * half, 4 * half + 4):
+                    nc.vector.scalar_tensor_tensor(
+                        out=xn[:, i, :],
+                        in0=x_sb[:, i, :],
+                        scalar=x_rstd[:, i : i + 1],
+                        in1=nw_b[:],
+                        op0=ALU.mult,
+                        op1=ALU.mult,
+                    )
+                for pair in range(2 * half, 2 * half + 2):
+                    xt = psum.tile([P, 4, P], F32, tag="read", bufs=READ_BANKS)
+                    for j in range(2):
+                        for u in range(2):
+                            nc.tensor.transpose(
+                                out=xt[:, 2 * j + u, :],
+                                in_=xn[:, 2 * pair + j, :].bitcast(F32)[:, u : D_MODEL // 2 : 2],
+                                identity=ident_f32[:],
+                            )
+                    x_turned.append(xt)
+            for half in range(2):
+                for pair in range(2 * half, 2 * half + 2):
+                    copy = nc.scalar.copy if half == 0 else nc.vector.tensor_copy
+                    copy(
+                        out=xg[:, 2 * pair : 2 * pair + 2, :, :].bitcast(F32),
+                        in_=x_turned[pair][:].rearrange("p (i u) t -> p i t u", u=2),
+                    )
+                four = slice(4 * half, 4 * half + 4)
+                nc.vector.quantize_mx(
+                    out=x_codes[:, four, :].rearrange("p i t -> p (i t)").bitcast(FP8X4),
+                    scales=x_scales[:, four, :].rearrange("p i t -> p (i t)"),
+                    in_=xg[:, four, :, :].rearrange("p i t w -> p (i t w)"),
                 )
-            nc.scalar.activation(out=x_std[:, four], in_=x_ms[:, four], func=ACT.Sqrt, bias=eps_sb[:, 0:1])
-        x_turned = []
-        for half in range(2):
-            four = slice(4 * half, 4 * half + 4)
-            nc.vector.reciprocal(out=x_rstd[:, four], in_=x_std[:, four])
-            for i in range(4 * half, 4 * half + 4):
-                nc.vector.scalar_tensor_tensor(
-                    out=xn[:, i, :],
-                    in0=x_sb[:, i, :],
-                    scalar=x_rstd[:, i : i + 1],
-                    in1=nw_b[:],
-                    op0=ALU.mult,
-                    op1=ALU.mult,
+            for i in range(TOKEN_TILES):
+                g_acc = psum.tile([P, BANK], F32, tag="read", bufs=READ_BANKS)
+                nc.tensor.matmul_mx(
+                    out=g_acc[:],
+                    lhsT=x_codes[:, i, :].bitcast(FP8X4),
+                    lhsT_scale=x_scales[:, i, :],
+                    rhs=gw_words[:].bitcast(FP8X4),
+                    rhs_scale=gw_planes[:],
+                    start=True,
+                    stop=True,
                 )
-            for pair in range(2 * half, 2 * half + 2):
-                xt = psum.tile([P, 4, P], F32, tag="read", bufs=READ_BANKS)
-                for j in range(2):
-                    for u in range(2):
-                        nc.tensor.transpose(
-                            out=xt[:, 2 * j + u, :],
-                            in_=xn[:, 2 * pair + j, :].bitcast(F32)[:, u : D_MODEL // 2 : 2],
-                            identity=ident_f32[:],
-                        )
-                x_turned.append(xt)
-        for half in range(2):
-            for pair in range(2 * half, 2 * half + 2):
-                copy = nc.scalar.copy if half == 0 else nc.vector.tensor_copy
-                copy(
-                    out=xg[:, 2 * pair : 2 * pair + 2, :, :].bitcast(F32),
-                    in_=x_turned[pair][:].rearrange("p (i u) t -> p i t u", u=2),
-                )
-            four = slice(4 * half, 4 * half + 4)
-            nc.vector.quantize_mx(
-                out=x_codes[:, four, :].rearrange("p i t -> p (i t)").bitcast(FP8X4),
-                scales=x_scales[:, four, :].rearrange("p i t -> p (i t)"),
-                in_=xg[:, four, :, :].rearrange("p i t w -> p (i t w)"),
+                nc.scalar.activation(out=gate_sb[:, i, :], in_=g_acc[:], func=ACT.Sigmoid)
+
+            for m in range(UNITS // 8):
+                qt_ps = psum.tile([P, 8, P], BF16, tag="turn", bufs=2)
+                for j in range(8):
+                    nc.tensor.transpose(
+                        out=qt_ps[:, j, :],
+                        in_=q_sb[:, 2 * m + j // HEADS, P * (j % HEADS) : P * (j % HEADS + 1)],
+                        identity=ident_bf16[:],
+                    )
+                nc.vector.tensor_copy(out=q_t[:, 8 * m : 8 * m + 8, :], in_=qt_ps[:])
+
+            nc.vector.tensor_copy(
+                out=w_sorted[:].bitcast(F32).rearrange("p (c u q) -> p c u q", c=BANKS, u=2),
+                in_=vw_raw[:].bitcast(F32).rearrange("p (c q u) -> p c u q", c=BANKS, u=2),
             )
-        for i in range(TOKEN_TILES):
-            g_acc = psum.tile([P, BANK], F32, tag="read", bufs=READ_BANKS)
-            nc.tensor.matmul_mx(
-                out=g_acc[:],
-                lhsT=x_codes[:, i, :].bitcast(FP8X4),
-                lhsT_scale=x_scales[:, i, :],
-                rhs=gw_words[:].bitcast(FP8X4),
-                rhs_scale=gw_planes[:],
-                start=True,
-                stop=True,
-            )
-            nc.scalar.activation(out=gate_sb[:, i, :], in_=g_acc[:], func=ACT.Sigmoid)
 
-        q_t = keep.tile([P, UNITS, P], BF16)
-        for m in range(UNITS // 8):
-            qt_ps = psum.tile([P, 8, P], BF16, tag="turn", bufs=2)
-            for j in range(8):
-                nc.tensor.transpose(
-                    out=qt_ps[:, j, :],
-                    in_=q_sb[:, 2 * m + j // HEADS, P * (j % HEADS) : P * (j % HEADS + 1)],
-                    identity=ident_bf16[:],
-                )
-            nc.vector.tensor_copy(out=q_t[:, 8 * m : 8 * m + 8, :], in_=qt_ps[:])
-
-        w_sorted = keep.tile([P, HEAD_V], BF16)
-        nc.vector.tensor_copy(
-            out=w_sorted[:].bitcast(F32).rearrange("p (c u q) -> p c u q", c=BANKS, u=2),
-            in_=vw_raw[:].bitcast(F32).rearrange("p (c q u) -> p c u q", c=BANKS, u=2),
-        )
-
+        work = ctx.enter_context(tc.tile_pool(name="work", bufs=3))
         out_tiles = out.rearrange("b (i p) d -> (b i) p d", p=P)
         r_banks = {}
         biases = {}
         stds = {}
         rstds = {}
+        weighed = {}
         normed = {}
         turned = {}
         groups = {}
@@ -223,6 +233,15 @@ def tile_glamemoryreader_pb_k_kernel(
                 accum_out=sums[:, u, c + 1 : c + 2],
             )
 
+        def weigh(u, c):
+            if not exists(u):
+                return
+            if c == 0:
+                y = work.tile([P, HEAD_V], F32, tag="y")
+                weighed[u] = y
+            cols = slice(BANK * c, BANK * (c + 1))
+            nc.vector.tensor_tensor(out=weighed[u][:, cols], in0=r_banks[(u, c)][:], in1=w_sorted[:, cols], op=ALU.mult)
+
         def partial(u):
             if not exists(u):
                 return
@@ -246,21 +265,14 @@ def tile_glamemoryreader_pb_k_kernel(
             nc.vector.reciprocal(out=rstd[:], in_=stds[u][:])
             rstds[u] = rstd
 
-        def normalise(u, c):
+        def normalise(u):
             if not exists(u):
                 return
-            if c == 0:
-                rn = work.tile([P, HEAD_V], BF16, tag="rn")
-                normed[u] = rn
-            cols = slice(BANK * c, BANK * (c + 1))
-            nc.vector.scalar_tensor_tensor(
-                out=normed[u][:, cols],
-                in0=r_banks[(u, c)][:],
-                scalar=rstds[u][:, 0:1],
-                in1=w_sorted[:, cols],
-                op0=ALU.mult,
-                op1=ALU.mult,
+            rn = work.tile([P, HEAD_V], BF16, tag="rn")
+            nc.gpsimd.tensor_scalar(
+                out=rn[:], in0=weighed[u][:], scalar1=rstds[u][:, 0:1], scalar2=1.0, op0=ALU.mult, op1=ALU.mult
             )
+            normed[u] = rn
 
         def transpose(u):
             if not exists(u):
@@ -290,21 +302,21 @@ def tile_glamemoryreader_pb_k_kernel(
             if not exists(u):
                 return
             code = work.tile([P, BANKS, P], U32, tag="code", align_bytes=64)
-            scale = work.tile([P, BANKS, P], U8, tag="scale", align_bytes=64)
+            plane = work.tile([P, BANKS, P], U8, tag="plane", align_bytes=64)
             nc.vector.quantize_mx(
                 out=code[:].rearrange("p c t -> p (c t)").bitcast(FP8X4),
-                scales=scale[:].rearrange("p c t -> p (c t)"),
+                scales=plane[:].rearrange("p c t -> p (c t)"),
                 in_=groups[u][:].rearrange("p c t w -> p (c t w)"),
             )
             codes[u] = code
-            scales[u] = scale
+            scales[u] = plane
 
         def project(u, c):
             if not exists(u):
                 return
             h = u % HEADS
             if h == 0 and c == 0:
-                acc = psum.tile([P, BANK], F32, tag="acc", bufs=1)
+                acc = psum.tile([P, BANK], F32, tag="acc", bufs=2)
                 accs[u // HEADS] = acc
             nc.tensor.matmul_mx(
                 out=accs[u // HEADS][:],
@@ -324,21 +336,25 @@ def tile_glamemoryreader_pb_k_kernel(
             nc.vector.tensor_tensor(out=o_sb[:], in0=accs[i][:], in1=gate_sb[:, i, :], op=ALU.mult)
             nc.sync.dma_start(out=out_tiles[i], in_=o_sb[:])
 
-        for u in range(-2, UNITS + 2):
-            regroup(u - 1, 0)
+        for u in range(-1, UNITS + 3):
+            finish(u - 3)
+            for c in range(BANKS - 2):
+                square(u, c + 1)
+                weigh(u, c)
+                read(u + 1, c)
+            square(u, BANKS - 1)
+            partial(u)
+            weigh(u, BANKS - 2)
+            read(u + 1, BANKS - 2)
+            root(u)
+            weigh(u, BANKS - 1)
+            transpose(u - 1)
+            read(u + 1, BANKS - 1)
             invert(u)
-            for c in range(BANKS - 1):
-                normalise(u, c)
-                read(u + 1, c + 1)
-                project(u - 2, c + 1)
-                square(u + 1, c + 1)
-            normalise(u, BANKS - 1)
-            read(u + 2, 0)
+            normalise(u)
+            quantise(u - 2)
+            square(u + 1, 0)
+            regroup(u - 1, 0)
             regroup(u - 1, 1)
-            partial(u + 1)
-            root(u + 1)
-            square(u + 2, 0)
-            transpose(u)
-            finish(u - 2)
-            quantise(u - 1)
-            project(u - 1, 0)
+            for c in range(BANKS):
+                project(u - 2, c)

@@ -336,25 +336,25 @@ def tile_glamemoryreader_pb_k_kernel(
             nc.vector.tensor_tensor(out=o_sb[:], in0=accs[i][:], in1=gate_sb[:, i, :], op=ALU.mult)
             nc.sync.dma_start(out=out_tiles[i], in_=o_sb[:])
 
-        for u in range(-1, UNITS + 3):
-            finish(u - 3)
-            for c in range(BANKS - 2):
+        for u in range(-1, UNITS + 5):
+            finish(u - 5)
+            for c in range(BANKS // 2):
                 square(u, c + 1)
                 weigh(u, c)
                 read(u + 1, c)
+                project(u - 4, 2 * c)
+                project(u - 4, 2 * c + 1)
             square(u, BANKS - 1)
             partial(u)
             weigh(u, BANKS - 2)
             read(u + 1, BANKS - 2)
             root(u)
             weigh(u, BANKS - 1)
-            transpose(u - 1)
             read(u + 1, BANKS - 1)
             invert(u)
             normalise(u)
-            quantise(u - 2)
+            quantise(u - 3)
             square(u + 1, 0)
-            regroup(u - 1, 0)
-            regroup(u - 1, 1)
-            for c in range(BANKS):
-                project(u - 2, c)
+            regroup(u - 2, 0)
+            regroup(u - 2, 1)
+            transpose(u - 1)

@@ -25,6 +25,7 @@ BANK = 512
 BANKS = HEAD_V // BANK
 UNITS = TOKEN_TILES * HEADS
 READ_BANKS = 4
+SCALAR_PASSES = 3
 EPS = 1e-5
 FLOPS = 2 * (1024 * 8192 * 512 + 1024 * 512 * 512 + 16 * 256 * 128 * 2048)
 
@@ -48,18 +49,16 @@ def tile_glamemoryreader_pb_k_kernel(
         psum = ctx.enter_context(tc.psum_pool(name="psum", bufs=1))
         ctx.enter_context(tc.manual_schedule())
 
-        ident_f32 = keep.tile([P, P], F32)
-        make_identity(nc, ident_f32[:])
         ident_bf16 = keep.tile([P, P], BF16)
         make_identity(nc, ident_bf16[:])
+        ident_f32 = keep.tile([P, P], F32)
+        make_identity(nc, ident_f32[:])
         eps_sb = keep.tile([P, 1], F32)
         nc.vector.memset(eps_sb[:], EPS)
         gw_planes = keep.tile([P, D_MODEL], U8, align_bytes=64)
         nc.vector.memset(gw_planes[:].bitcast(I32), 0)
         ow_planes = keep.tile([P, HEADS * BANKS, D_MODEL], U8, align_bytes=64)
-        nc.vector.memset(ow_planes[:].bitcast(I32), 0)
         sums = keep.tile([P, UNITS, 8], F32)
-        nc.vector.memset(sums[:], EPS)
 
         gate_sb = keep.tile([P, TOKEN_TILES, D_MODEL], F32)
         q_t = keep.tile([P, UNITS, P], BF16)
@@ -70,14 +69,22 @@ def tile_glamemoryreader_pb_k_kernel(
         ]
 
         with tc.tile_pool(name="front", bufs=1) as front:
+            ones = front.tile([P, P], BF16)
+            nc.vector.memset(ones[:], 1.0)
+            nw_row = front.tile([P, D_MODEL], BF16)
+            nc.vector.memset(nw_row[:].bitcast(I32), 0)
+            nc.vector.memset(ow_planes[:].bitcast(I32), 0)
+            nc.vector.memset(sums[:], EPS)
+
             x_sb = front.tile([P, TOKEN_TILES, D_MODEL], BF16)
             x_dram = hidden_states.rearrange("b (i p) d -> p (b i) d", p=P)
-            for half in range(2):
-                four = slice(4 * half, 4 * half + 4)
-                nc.sync.dma_start(out=x_sb[:, four, :], in_=x_dram[:, four, :])
-            nw_b = front.tile([P, D_MODEL], BF16)
-            nc.sync.dma_start(out=nw_b[:], in_=norm_w.partition_broadcast(P))
+            q_sb = front.tile([P, TOKEN_TILES, HEADS * P], BF16)
             gw_words = front.tile([P, D_MODEL], U32, align_bytes=64)
+            vw_raw = front.tile([P, HEAD_V], BF16)
+
+            nc.sync.dma_start(out=nw_row[0:1, :], in_=norm_w.unsqueeze(0))
+            for b in range(BATCH):
+                nc.sync.dma_start(out=x_sb[:, 2 * b : 2 * b + 2, :], in_=x_dram[:, 2 * b : 2 * b + 2, :])
             nc.sync.dma_start(
                 out=gw_words[:].bitcast(I32),
                 in_=gate_w_words[0].rearrange("p n t -> p (n t)").bitcast(I32),
@@ -86,11 +93,9 @@ def tile_glamemoryreader_pb_k_kernel(
                 nc.sync.dma_start(
                     out=gw_planes[r:P:32, :].bitcast(I32), in_=gate_w_scales[0, r:16:4, :].bitcast(I32)
                 )
-            q_sb = front.tile([P, TOKEN_TILES, HEADS * P], BF16)
-            nc.sync.dma_start(out=q_sb[:], in_=q_hat.rearrange("b (i p) h k -> p (b i) (h k)", p=P))
-            vw_raw = front.tile([P, HEAD_V], BF16)
-            nc.sync.dma_start(out=state[0][:], in_=recurrent_state[0, 0])
             nc.sync.dma_start(out=vw_raw[:], in_=v_norm_w.partition_broadcast(P))
+            nc.sync.dma_start(out=q_sb[:], in_=q_hat.rearrange("b (i p) h k -> p (b i) (h k)", p=P))
+            nc.sync.dma_start(out=state[0][:], in_=recurrent_state[0, 0])
             for r in range(4):
                 nc.sync.dma_start(
                     out=ow_planes[r:P:32, :, :].bitcast(I32),
@@ -107,6 +112,19 @@ def tile_glamemoryreader_pb_k_kernel(
                 for h in range(HEADS):
                     nc.sync.dma_start(out=state[HEADS * b + h][:], in_=recurrent_state[b, h])
 
+            def turn_queries(b):
+                qt_ps = psum.tile([P, 2 * HEADS, P], BF16, tag="acc", bufs=2)
+                for j in range(2 * HEADS):
+                    nc.tensor.transpose(
+                        out=qt_ps[:, j, :],
+                        in_=q_sb[:, 2 * b + j // HEADS, P * (j % HEADS) : P * (j % HEADS + 1)],
+                        identity=ident_bf16[:],
+                    )
+                nc.vector.tensor_copy(out=q_t[:, 2 * HEADS * b : 2 * HEADS * (b + 1), :], in_=qt_ps[:])
+
+            nw_ps = psum.tile([P, D_MODEL], F32, tag="acc", bufs=2)
+            nc.tensor.matmul(out=nw_ps[:], lhsT=ones[:], rhs=nw_row[:], start=True, stop=True)
+
             x_ms = front.tile([P, TOKEN_TILES], F32)
             x_std = front.tile([P, TOKEN_TILES], F32)
             x_rstd = front.tile([P, TOKEN_TILES], F32)
@@ -114,9 +132,14 @@ def tile_glamemoryreader_pb_k_kernel(
             xg = front.tile([P, TOKEN_TILES, P, 4], BF16, align_bytes=64)
             x_codes = front.tile([P, TOKEN_TILES, P], U32, align_bytes=64)
             x_scales = front.tile([P, TOKEN_TILES, P], U8, align_bytes=64)
-            for half in range(2):
-                four = slice(4 * half, 4 * half + 4)
-                for i in range(4 * half, 4 * half + 4):
+            x_turned = {}
+
+            def is_pair(b):
+                return 0 <= b < BATCH
+
+            def x_stats(b):
+                two = slice(2 * b, 2 * b + 2)
+                for i in range(2 * b, 2 * b + 2):
                     x_sq = front.tile([P, BANK], BF16, tag="x_sq", bufs=4)
                     nc.scalar.activation(
                         out=x_sq[:],
@@ -125,70 +148,76 @@ def tile_glamemoryreader_pb_k_kernel(
                         scale=D_MODEL**-0.5,
                         accum_out=x_ms[:, i : i + 1],
                     )
-                nc.scalar.activation(out=x_std[:, four], in_=x_ms[:, four], func=ACT.Sqrt, bias=eps_sb[:, 0:1])
-            x_turned = []
-            for half in range(2):
-                four = slice(4 * half, 4 * half + 4)
-                nc.vector.reciprocal(out=x_rstd[:, four], in_=x_std[:, four])
-                for i in range(4 * half, 4 * half + 4):
+                nc.scalar.activation(out=x_std[:, two], in_=x_ms[:, two], func=ACT.Sqrt, bias=eps_sb[:, 0:1])
+
+            def x_normalise(b):
+                if not is_pair(b):
+                    return
+                two = slice(2 * b, 2 * b + 2)
+                nc.vector.reciprocal(out=x_rstd[:, two], in_=x_std[:, two])
+                for i in range(2 * b, 2 * b + 2):
                     nc.vector.scalar_tensor_tensor(
                         out=xn[:, i, :],
                         in0=x_sb[:, i, :],
                         scalar=x_rstd[:, i : i + 1],
-                        in1=nw_b[:],
+                        in1=nw_ps[:],
                         op0=ALU.mult,
                         op1=ALU.mult,
                     )
-                for pair in range(2 * half, 2 * half + 2):
-                    xt = psum.tile([P, 4, P], F32, tag="read", bufs=READ_BANKS)
-                    for j in range(2):
-                        for u in range(2):
-                            nc.tensor.transpose(
-                                out=xt[:, 2 * j + u, :],
-                                in_=xn[:, 2 * pair + j, :].bitcast(F32)[:, u : D_MODEL // 2 : 2],
-                                identity=ident_f32[:],
-                            )
-                    x_turned.append(xt)
-            for half in range(2):
-                for pair in range(2 * half, 2 * half + 2):
-                    copy = nc.scalar.copy if half == 0 else nc.vector.tensor_copy
-                    copy(
-                        out=xg[:, 2 * pair : 2 * pair + 2, :, :].bitcast(F32),
-                        in_=x_turned[pair][:].rearrange("p (i u) t -> p i t u", u=2),
-                    )
-                four = slice(4 * half, 4 * half + 4)
-                nc.vector.quantize_mx(
-                    out=x_codes[:, four, :].rearrange("p i t -> p (i t)").bitcast(FP8X4),
-                    scales=x_scales[:, four, :].rearrange("p i t -> p (i t)"),
-                    in_=xg[:, four, :, :].rearrange("p i t w -> p (i t w)"),
-                )
-            for i in range(TOKEN_TILES):
-                g_acc = psum.tile([P, BANK], F32, tag="read", bufs=READ_BANKS)
-                nc.tensor.matmul_mx(
-                    out=g_acc[:],
-                    lhsT=x_codes[:, i, :].bitcast(FP8X4),
-                    lhsT_scale=x_scales[:, i, :],
-                    rhs=gw_words[:].bitcast(FP8X4),
-                    rhs_scale=gw_planes[:],
-                    start=True,
-                    stop=True,
-                )
-                nc.scalar.activation(out=gate_sb[:, i, :], in_=g_acc[:], func=ACT.Sigmoid)
+                xt = psum.tile([P, 4, P], F32, tag="turn", bufs=2)
+                for j in range(2):
+                    for u in range(2):
+                        nc.tensor.transpose(
+                            out=xt[:, 2 * j + u, :],
+                            in_=xn[:, 2 * b + j, :].bitcast(F32)[:, u : D_MODEL // 2 : 2],
+                            identity=ident_f32[:],
+                        )
+                x_turned[b] = xt
 
-            for m in range(UNITS // 8):
-                qt_ps = psum.tile([P, 8, P], BF16, tag="turn", bufs=2)
-                for j in range(8):
-                    nc.tensor.transpose(
-                        out=qt_ps[:, j, :],
-                        in_=q_sb[:, 2 * m + j // HEADS, P * (j % HEADS) : P * (j % HEADS + 1)],
-                        identity=ident_bf16[:],
+            def x_quantise(b):
+                if not is_pair(b):
+                    return
+                two = slice(2 * b, 2 * b + 2)
+                nc.vector.tensor_copy(
+                    out=xg[:, two, :, :].bitcast(F32), in_=x_turned[b][:].rearrange("p (i u) t -> p i t u", u=2)
+                )
+                nc.vector.quantize_mx(
+                    out=x_codes[:, two, :].rearrange("p i t -> p (i t)").bitcast(FP8X4),
+                    scales=x_scales[:, two, :].rearrange("p i t -> p (i t)"),
+                    in_=xg[:, two, :, :].rearrange("p i t w -> p (i t w)"),
+                )
+
+            def gate(b):
+                if not is_pair(b):
+                    return
+                for i in range(2 * b, 2 * b + 2):
+                    g_acc = psum.tile([P, BANK], F32, tag="read", bufs=READ_BANKS)
+                    nc.tensor.matmul_mx(
+                        out=g_acc[:],
+                        lhsT=x_codes[:, i, :].bitcast(FP8X4),
+                        lhsT_scale=x_scales[:, i, :],
+                        rhs=gw_words[:].bitcast(FP8X4),
+                        rhs_scale=gw_planes[:],
+                        start=True,
+                        stop=True,
                     )
-                nc.vector.tensor_copy(out=q_t[:, 8 * m : 8 * m + 8, :], in_=qt_ps[:])
+                    nc.scalar.activation(out=gate_sb[:, i, :], in_=g_acc[:], func=ACT.Sigmoid)
+
+            for b in range(BATCH):
+                x_stats(b)
+            for b in range(BATCH + 1):
+                x_normalise(b)
+                x_quantise(b - 1)
+                gate(b - 1)
+            warm = front.tile([P, 1], F32)
+            nc.scalar.activation(out=warm[:], in_=eps_sb[:], func=ACT.Sqrt)
 
             nc.vector.tensor_copy(
                 out=w_sorted[:].bitcast(F32).rearrange("p (c u q) -> p c u q", c=BANKS, u=2),
                 in_=vw_raw[:].bitcast(F32).rearrange("p (c q u) -> p c u q", c=BANKS, u=2),
             )
+            for b in range(BATCH):
+                turn_queries(b)
 
         work = ctx.enter_context(tc.tile_pool(name="work", bufs=3))
         out_tiles = out.rearrange("b (i p) d -> (b i) p d", p=P)
@@ -201,7 +230,7 @@ def tile_glamemoryreader_pb_k_kernel(
         turned = {}
         groups = {}
         codes = {}
-        scales = {}
+        planes = {}
         accs = {}
 
         def exists(u):
@@ -286,16 +315,16 @@ def tile_glamemoryreader_pb_k_kernel(
                     )
                 turned[(u, m)] = rt
 
-        def regroup(u, m):
+        def regroup(u, copy, first, last):
             if not exists(u):
                 return
-            if m == 0:
+            if first == 0:
                 grouped = work.tile([P, BANKS, P, 4], BF16, tag="grouped", align_bytes=64)
                 groups[u] = grouped
-            copy = nc.scalar.copy if m == 0 else nc.vector.tensor_copy
+            bank = turned[(u, first // 2)]
             copy(
-                out=groups[u][:, 2 * m : 2 * m + 2, :, :].bitcast(F32),
-                in_=turned[(u, m)][:].rearrange("p (c u) t -> p c t u", u=2),
+                out=groups[u][:, first : last + 1, :, :].bitcast(F32),
+                in_=bank[:, 2 * (first % 2) : 2 * (last % 2) + 2, :].rearrange("p (c u) t -> p c t u", u=2),
             )
 
         def quantise(u):
@@ -309,7 +338,7 @@ def tile_glamemoryreader_pb_k_kernel(
                 in_=groups[u][:].rearrange("p c t w -> p (c t w)"),
             )
             codes[u] = code
-            scales[u] = plane
+            planes[u] = plane
 
         def project(u, c):
             if not exists(u):
@@ -321,7 +350,7 @@ def tile_glamemoryreader_pb_k_kernel(
             nc.tensor.matmul_mx(
                 out=accs[u // HEADS][:],
                 lhsT=codes[u][:, c, :].bitcast(FP8X4),
-                lhsT_scale=scales[u][:, c, :],
+                lhsT_scale=planes[u][:, c, :],
                 rhs=ow_words[h][:, c, :].bitcast(FP8X4),
                 rhs_scale=ow_planes[:, BANKS * h + c, :],
                 start=(h == 0 and c == 0),
@@ -339,22 +368,23 @@ def tile_glamemoryreader_pb_k_kernel(
         for u in range(-1, UNITS + 5):
             finish(u - 5)
             for c in range(BANKS // 2):
-                square(u, c + 1)
+                square(u, c + 2)
                 weigh(u, c)
                 read(u + 1, c)
                 project(u - 4, 2 * c)
                 project(u - 4, 2 * c + 1)
-            square(u, BANKS - 1)
             partial(u)
-            weigh(u, BANKS - 2)
-            read(u + 1, BANKS - 2)
+            regroup(u - 2, nc.scalar.copy, 0, 1)
+            weigh(u, 2)
+            read(u + 1, 2)
             root(u)
-            weigh(u, BANKS - 1)
-            read(u + 1, BANKS - 1)
+            regroup(u - 2, nc.scalar.copy, 2, SCALAR_PASSES - 1)
+            weigh(u, 3)
+            read(u + 1, 3)
+            square(u + 1, 0)
+            square(u + 1, 1)
             invert(u)
             normalise(u)
             quantise(u - 3)
-            square(u + 1, 0)
-            regroup(u - 2, 0)
-            regroup(u - 2, 1)
+            regroup(u - 2, nc.vector.tensor_copy, SCALAR_PASSES, BANKS - 1)
             transpose(u - 1)

@@ -126,7 +126,6 @@ def tile_glamemoryreader_pb_k_kernel(
             nc.tensor.matmul(out=nw_ps[:], lhsT=ones[:], rhs=nw_row[:], start=True, stop=True)
 
             x_ms = front.tile([P, TOKEN_TILES], F32)
-            x_std = front.tile([P, TOKEN_TILES], F32)
             x_rstd = front.tile([P, TOKEN_TILES], F32)
             xn = front.tile([P, TOKEN_TILES, D_MODEL], BF16)
             xg = front.tile([P, TOKEN_TILES, P, 4], BF16, align_bytes=64)
@@ -148,13 +147,14 @@ def tile_glamemoryreader_pb_k_kernel(
                         scale=D_MODEL**-0.5,
                         accum_out=x_ms[:, i : i + 1],
                     )
-                nc.scalar.activation(out=x_std[:, two], in_=x_ms[:, two], func=ACT.Sqrt, bias=eps_sb[:, 0:1])
+                nc.scalar.activation(
+                    out=x_rstd[:, two], in_=x_ms[:, two], func=ACT.Abs_reciprocal_sqrt, bias=eps_sb[:, 0:1]
+                )
 
             def x_normalise(b):
                 if not is_pair(b):
                     return
                 two = slice(2 * b, 2 * b + 2)
-                nc.vector.reciprocal(out=x_rstd[:, two], in_=x_std[:, two])
                 for i in range(2 * b, 2 * b + 2):
                     nc.vector.scalar_tensor_tensor(
                         out=xn[:, i, :],
@@ -210,7 +210,7 @@ def tile_glamemoryreader_pb_k_kernel(
                 x_quantise(b - 1)
                 gate(b - 1)
             warm = front.tile([P, 1], F32)
-            nc.scalar.activation(out=warm[:], in_=eps_sb[:], func=ACT.Sqrt)
+            nc.scalar.activation(out=warm[:], in_=eps_sb[:], func=ACT.Abs_reciprocal_sqrt)
 
             nc.vector.tensor_copy(
                 out=w_sorted[:].bitcast(F32).rearrange("p (c u q) -> p c u q", c=BANKS, u=2),
@@ -223,7 +223,6 @@ def tile_glamemoryreader_pb_k_kernel(
         out_tiles = out.rearrange("b (i p) d -> (b i) p d", p=P)
         r_banks = {}
         biases = {}
-        stds = {}
         rstds = {}
         weighed = {}
         normed = {}
@@ -281,17 +280,13 @@ def tile_glamemoryreader_pb_k_kernel(
         def root(u):
             if not exists(u):
                 return
-            std = work.tile([P, 1], F32, tag="std", bufs=4)
-            nc.scalar.activation(
-                out=std[:], in_=sums[:, u, BANKS : BANKS + 1], func=ACT.Sqrt, bias=biases[u][:, 0:1]
-            )
-            stds[u] = std
-
-        def invert(u):
-            if not exists(u):
-                return
             rstd = work.tile([P, 1], F32, tag="rstd", bufs=4)
-            nc.vector.reciprocal(out=rstd[:], in_=stds[u][:])
+            nc.scalar.activation(
+                out=rstd[:],
+                in_=sums[:, u, BANKS : BANKS + 1],
+                func=ACT.Abs_reciprocal_sqrt,
+                bias=biases[u][:, 0:1],
+            )
             rstds[u] = rstd
 
         def normalise(u):
@@ -383,7 +378,6 @@ def tile_glamemoryreader_pb_k_kernel(
             read(u + 1, 3)
             square(u + 1, 0)
             square(u + 1, 1)
-            invert(u)
             normalise(u)
             quantise(u - 3)
             regroup(u - 2, nc.vector.tensor_copy, SCALAR_PASSES, BANKS - 1)

@@ -24,6 +24,8 @@ TILES_PER_BATCH = SEQ // P
 BANK = 512
 BANKS = HEAD_V // BANK
 UNITS = TOKEN_TILES * HEADS
+STATE_BUFS = 12
+POW_UNITS = 3
 READ_BANKS = 4
 SCALAR_PASSES = 3
 EPS = 1e-5
@@ -55,6 +57,8 @@ def tile_glamemoryreader_pb_k_kernel(
         make_identity(nc, ident_f32[:])
         eps_sb = keep.tile([P, 1], F32)
         nc.vector.memset(eps_sb[:], EPS)
+        minus_half = keep.tile([P, 1], F32)
+        nc.vector.memset(minus_half[:], -0.5)
         gw_planes = keep.tile([P, D_MODEL], U8, align_bytes=64)
         nc.vector.memset(gw_planes[:].bitcast(I32), 0)
         ow_planes = keep.tile([P, HEADS * BANKS, D_MODEL], U8, align_bytes=64)
@@ -63,161 +67,220 @@ def tile_glamemoryreader_pb_k_kernel(
         gate_sb = keep.tile([P, TOKEN_TILES, D_MODEL], F32)
         q_t = keep.tile([P, UNITS, P], BF16)
         w_sorted = keep.tile([P, HEAD_V], BF16)
-        state = [keep.tile([P, HEAD_V], BF16, name="state_%d" % bh) for bh in range(BATCH * HEADS)]
         ow_words = [
             keep.tile([P, BANKS, D_MODEL], U32, name="ow_words_%d" % h, align_bytes=64) for h in range(HEADS)
         ]
 
-        with tc.tile_pool(name="front", bufs=1) as front:
-            ones = front.tile([P, P], BF16)
-            nc.vector.memset(ones[:], 1.0)
-            nw_row = front.tile([P, D_MODEL], BF16)
-            nc.vector.memset(nw_row[:].bitcast(I32), 0)
-            nc.vector.memset(ow_planes[:].bitcast(I32), 0)
-            nc.vector.memset(sums[:], EPS)
+        ones = keep.tile([P, P], BF16)
+        nc.vector.memset(ones[:], 1.0)
+        nw_row = keep.tile([P, D_MODEL], BF16)
+        nc.vector.memset(nw_row[:].bitcast(I32), 0)
+        nc.vector.memset(ow_planes[:].bitcast(I32), 0)
+        nc.vector.memset(sums[:], EPS)
 
-            x_sb = front.tile([P, TOKEN_TILES, D_MODEL], BF16)
-            x_dram = hidden_states.rearrange("b (i p) d -> p (b i) d", p=P)
-            q_sb = front.tile([P, TOKEN_TILES, HEADS * P], BF16)
-            gw_words = front.tile([P, D_MODEL], U32, align_bytes=64)
-            vw_raw = front.tile([P, HEAD_V], BF16)
+        x_sb = keep.tile([P, TOKEN_TILES, D_MODEL], BF16)
+        x_dram = hidden_states.rearrange("b (i p) d -> p (b i) d", p=P)
+        q_sb = keep.tile([P, TOKEN_TILES, HEADS * P], BF16)
+        q_dram = q_hat.rearrange("b (i p) h k -> p (b i) (h k)", p=P)
+        gw_words = keep.tile([P, D_MODEL], U32, align_bytes=64)
+        vw_raw = keep.tile([P, HEAD_V], BF16)
 
-            nc.sync.dma_start(out=nw_row[0:1, :], in_=norm_w.unsqueeze(0))
-            for b in range(BATCH):
-                nc.sync.dma_start(out=x_sb[:, 2 * b : 2 * b + 2, :], in_=x_dram[:, 2 * b : 2 * b + 2, :])
+        states = {}
+
+        def load_state(bh):
+            state = keep.tile([P, HEAD_V], BF16, tag="state", bufs=STATE_BUFS)
+            nc.sync.dma_start(out=state[:], in_=recurrent_state[bh // HEADS, bh % HEADS])
+            states[bh] = state
+
+        def load_x(b):
+            nc.sync.dma_start(out=x_sb[:, 2 * b : 2 * b + 2, :], in_=x_dram[:, 2 * b : 2 * b + 2, :])
+
+        def load_q(first, last):
+            nc.sync.dma_start(out=q_sb[:, 2 * first : 2 * last + 2, :], in_=q_dram[:, 2 * first : 2 * last + 2, :])
+
+        load_x(0)
+        nc.sync.dma_start(out=nw_row[0:1, :], in_=norm_w.unsqueeze(0))
+        for b in range(1, BATCH):
+            load_x(b)
+        load_q(0, 0)
+        load_state(0)
+        nc.sync.dma_start(out=vw_raw[:], in_=v_norm_w.partition_broadcast(P))
+        nc.sync.dma_start(
+            out=gw_words[:].bitcast(I32),
+            in_=gate_w_words[0].rearrange("p n t -> p (n t)").bitcast(I32),
+        )
+        for r in range(4):
+            nc.sync.dma_start(out=gw_planes[r:P:32, :].bitcast(I32), in_=gate_w_scales[0, r:16:4, :].bitcast(I32))
+        load_state(1)
+        load_q(1, BATCH - 1)
+        load_state(2)
+        load_state(3)
+        for r in range(4):
             nc.sync.dma_start(
-                out=gw_words[:].bitcast(I32),
-                in_=gate_w_words[0].rearrange("p n t -> p (n t)").bitcast(I32),
+                out=ow_planes[r:P:32, :, :].bitcast(I32),
+                in_=o_w_scales[:, r:16:4, :].rearrange("g c n -> c g n").bitcast(I32),
             )
-            for r in range(4):
-                nc.sync.dma_start(
-                    out=gw_planes[r:P:32, :].bitcast(I32), in_=gate_w_scales[0, r:16:4, :].bitcast(I32)
+        for h in range(HEADS):
+            nc.sync.dma_start(
+                out=ow_words[h][:].bitcast(I32),
+                in_=o_w_words[BANKS * h : BANKS * (h + 1)].rearrange("g p n t -> p g (n t)").bitcast(I32),
+            )
+        for bh in range(HEADS, STATE_BUFS):
+            load_state(bh)
+
+        q_turned = {}
+
+        def turn_queries(b):
+            if not 0 <= b < BATCH:
+                return
+            qt_ps = psum.tile([P, 2 * HEADS, P], BF16, tag="turn", bufs=2)
+            for j in range(2 * HEADS):
+                nc.tensor.transpose(
+                    out=qt_ps[:, j, :],
+                    in_=q_sb[:, 2 * b + j // HEADS, P * (j % HEADS) : P * (j % HEADS + 1)],
+                    identity=ident_bf16[:],
                 )
-            nc.sync.dma_start(out=vw_raw[:], in_=v_norm_w.partition_broadcast(P))
-            nc.sync.dma_start(out=q_sb[:], in_=q_hat.rearrange("b (i p) h k -> p (b i) (h k)", p=P))
-            nc.sync.dma_start(out=state[0][:], in_=recurrent_state[0, 0])
-            for r in range(4):
-                nc.sync.dma_start(
-                    out=ow_planes[r:P:32, :, :].bitcast(I32),
-                    in_=o_w_scales[:, r:16:4, :].rearrange("g c n -> c g n").bitcast(I32),
-                )
-            for h in range(HEADS):
-                if h > 0:
-                    nc.sync.dma_start(out=state[h][:], in_=recurrent_state[0, h])
-                nc.sync.dma_start(
-                    out=ow_words[h][:].bitcast(I32),
-                    in_=o_w_words[BANKS * h : BANKS * (h + 1)].rearrange("g p n t -> p g (n t)").bitcast(I32),
-                )
-            for b in range(1, BATCH):
-                for h in range(HEADS):
-                    nc.sync.dma_start(out=state[HEADS * b + h][:], in_=recurrent_state[b, h])
+            q_turned[b] = qt_ps
 
-            def turn_queries(b):
-                qt_ps = psum.tile([P, 2 * HEADS, P], BF16, tag="acc", bufs=2)
-                for j in range(2 * HEADS):
-                    nc.tensor.transpose(
-                        out=qt_ps[:, j, :],
-                        in_=q_sb[:, 2 * b + j // HEADS, P * (j % HEADS) : P * (j % HEADS + 1)],
-                        identity=ident_bf16[:],
-                    )
-                nc.vector.tensor_copy(out=q_t[:, 2 * HEADS * b : 2 * HEADS * (b + 1), :], in_=qt_ps[:])
+        def keep_queries(b, copy):
+            if 0 <= b < BATCH:
+                copy(out=q_t[:, 2 * HEADS * b : 2 * HEADS * (b + 1), :], in_=q_turned[b][:])
 
-            nw_ps = psum.tile([P, D_MODEL], F32, tag="acc", bufs=2)
-            nc.tensor.matmul(out=nw_ps[:], lhsT=ones[:], rhs=nw_row[:], start=True, stop=True)
+        nw_ps = psum.tile([P, D_MODEL], F32, tag="acc", bufs=2)
+        nc.tensor.matmul(out=nw_ps[:], lhsT=ones[:], rhs=nw_row[:], start=True, stop=True)
 
-            x_ms = front.tile([P, TOKEN_TILES], F32)
-            x_rstd = front.tile([P, TOKEN_TILES], F32)
-            xn = front.tile([P, TOKEN_TILES, D_MODEL], BF16)
-            xg = front.tile([P, TOKEN_TILES, P, 4], BF16, align_bytes=64)
-            x_codes = front.tile([P, TOKEN_TILES, P], U32, align_bytes=64)
-            x_scales = front.tile([P, TOKEN_TILES, P], U8, align_bytes=64)
-            x_turned = {}
+        warm = keep.tile([P, 2], F32)
+        nc.scalar.activation(out=warm[:, 0:1], in_=eps_sb[:], func=ACT.Abs_reciprocal_sqrt)
+        x_rstd = keep.tile([P, TOKEN_TILES], F32)
+        x_normed = {}
+        x_grouped = {}
+        x_codes = keep.tile([P, TOKEN_TILES, P], U32, align_bytes=64)
+        x_scales = keep.tile([P, TOKEN_TILES, P], U8, align_bytes=64)
+        x_turned = {}
 
-            def is_pair(b):
-                return 0 <= b < BATCH
+        def is_pair(b):
+            return 0 <= b < BATCH
 
-            def x_stats(b):
-                two = slice(2 * b, 2 * b + 2)
-                for i in range(2 * b, 2 * b + 2):
-                    x_sq = front.tile([P, BANK], BF16, tag="x_sq", bufs=4)
+        def x_stats(b):
+            two = slice(2 * b, 2 * b + 2)
+            x_ms = keep.tile([P, 2], F32, tag="x_ms_%d" % b, bufs=1)
+            for j in range(2):
+                x_sq = keep.tile([P, BANK], BF16, tag="x_sq_%d" % j, bufs=2)
+                x_tile = x_sb[:, 2 * b + j, :]
+                if j == 0 or b >= 2:
                     nc.scalar.activation(
                         out=x_sq[:],
-                        in_=x_sb[:, i, :],
+                        in_=x_tile,
                         func=ACT.Square,
                         scale=D_MODEL**-0.5,
-                        accum_out=x_ms[:, i : i + 1],
+                        accum_out=x_ms[:, j : j + 1],
                     )
-                nc.scalar.activation(
-                    out=x_rstd[:, two], in_=x_ms[:, two], func=ACT.Abs_reciprocal_sqrt, bias=eps_sb[:, 0:1]
-                )
-
-            def x_normalise(b):
-                if not is_pair(b):
-                    return
-                two = slice(2 * b, 2 * b + 2)
-                for i in range(2 * b, 2 * b + 2):
+                else:
                     nc.vector.scalar_tensor_tensor(
-                        out=xn[:, i, :],
-                        in0=x_sb[:, i, :],
-                        scalar=x_rstd[:, i : i + 1],
-                        in1=nw_ps[:],
+                        out=x_sq[:],
+                        in0=x_tile,
+                        scalar=1.0 / D_MODEL,
+                        in1=x_tile,
                         op0=ALU.mult,
                         op1=ALU.mult,
+                        accum_out=x_ms[:, j : j + 1],
                     )
-                xt = psum.tile([P, 4, P], F32, tag="turn", bufs=2)
-                for j in range(2):
-                    for u in range(2):
-                        nc.tensor.transpose(
-                            out=xt[:, 2 * j + u, :],
-                            in_=xn[:, 2 * b + j, :].bitcast(F32)[:, u : D_MODEL // 2 : 2],
-                            identity=ident_f32[:],
-                        )
-                x_turned[b] = xt
-
-            def x_quantise(b):
-                if not is_pair(b):
-                    return
-                two = slice(2 * b, 2 * b + 2)
-                nc.vector.tensor_copy(
-                    out=xg[:, two, :, :].bitcast(F32), in_=x_turned[b][:].rearrange("p (i u) t -> p i t u", u=2)
-                )
-                nc.vector.quantize_mx(
-                    out=x_codes[:, two, :].rearrange("p i t -> p (i t)").bitcast(FP8X4),
-                    scales=x_scales[:, two, :].rearrange("p i t -> p (i t)"),
-                    in_=xg[:, two, :, :].rearrange("p i t w -> p (i t w)"),
-                )
-
-            def gate(b):
-                if not is_pair(b):
-                    return
-                for i in range(2 * b, 2 * b + 2):
-                    g_acc = psum.tile([P, BANK], F32, tag="read", bufs=READ_BANKS)
-                    nc.tensor.matmul_mx(
-                        out=g_acc[:],
-                        lhsT=x_codes[:, i, :].bitcast(FP8X4),
-                        lhsT_scale=x_scales[:, i, :],
-                        rhs=gw_words[:].bitcast(FP8X4),
-                        rhs_scale=gw_planes[:],
-                        start=True,
-                        stop=True,
-                    )
-                    nc.scalar.activation(out=gate_sb[:, i, :], in_=g_acc[:], func=ACT.Sigmoid)
-
-            for b in range(BATCH):
-                x_stats(b)
-            for b in range(BATCH + 1):
-                x_normalise(b)
-                x_quantise(b - 1)
-                gate(b - 1)
-            warm = front.tile([P, 1], F32)
-            nc.scalar.activation(out=warm[:], in_=eps_sb[:], func=ACT.Abs_reciprocal_sqrt)
-
-            nc.vector.tensor_copy(
-                out=w_sorted[:].bitcast(F32).rearrange("p (c u q) -> p c u q", c=BANKS, u=2),
-                in_=vw_raw[:].bitcast(F32).rearrange("p (c q u) -> p c u q", c=BANKS, u=2),
+            nc.scalar.activation(
+                out=x_rstd[:, two], in_=x_ms[:], func=ACT.Abs_reciprocal_sqrt, bias=eps_sb[:, 0:1]
             )
-            for b in range(BATCH):
-                turn_queries(b)
+
+        def x_normalise(b):
+            if not is_pair(b):
+                return
+            xn = keep.tile([P, 2, D_MODEL], BF16, tag="xn", bufs=2)
+            for j in range(2):
+                i = 2 * b + j
+                nc.vector.scalar_tensor_tensor(
+                    out=xn[:, j, :],
+                    in0=x_sb[:, i, :],
+                    scalar=x_rstd[:, i : i + 1],
+                    in1=nw_ps[:],
+                    op0=ALU.mult,
+                    op1=ALU.mult,
+                )
+            x_normed[b] = xn
+
+        def x_turn(b):
+            if not is_pair(b):
+                return
+            xt = psum.tile([P, 4, P], F32, tag="turn", bufs=2)
+            for j in range(2):
+                for u in range(2):
+                    nc.tensor.transpose(
+                        out=xt[:, 2 * j + u, :],
+                        in_=x_normed[b][:, j, :].bitcast(F32)[:, u : D_MODEL // 2 : 2],
+                        identity=ident_f32[:],
+                    )
+            x_turned[b] = xt
+
+        def x_regroup(b, copy):
+            if not is_pair(b):
+                return
+            xg = keep.tile([P, 2, P, 4], BF16, tag="xg", bufs=2, align_bytes=64)
+            copy(out=xg[:].bitcast(F32), in_=x_turned[b][:].rearrange("p (i u) t -> p i t u", u=2))
+            x_grouped[b] = xg
+
+        def x_quantise(b):
+            if not is_pair(b):
+                return
+            two = slice(2 * b, 2 * b + 2)
+            nc.vector.quantize_mx(
+                out=x_codes[:, two, :].rearrange("p i t -> p (i t)").bitcast(FP8X4),
+                scales=x_scales[:, two, :].rearrange("p i t -> p (i t)"),
+                in_=x_grouped[b][:].rearrange("p i t w -> p (i t w)"),
+            )
+
+        g_accs = {}
+
+        def gate(i):
+            if not 0 <= i < TOKEN_TILES:
+                return
+            g_acc = psum.tile([P, BANK], F32, tag="acc", bufs=2)
+            nc.tensor.matmul_mx(
+                out=g_acc[:],
+                lhsT=x_codes[:, i, :].bitcast(FP8X4),
+                lhsT_scale=x_scales[:, i, :],
+                rhs=gw_words[:].bitcast(FP8X4),
+                rhs_scale=gw_planes[:],
+                start=True,
+                stop=True,
+            )
+            g_accs[i] = g_acc
+
+        def gate_out(i):
+            if 0 <= i < TOKEN_TILES:
+                nc.scalar.activation(out=gate_sb[:, i, :], in_=g_accs[i][:], func=ACT.Sigmoid)
+
+        for b in range(BATCH):
+            x_stats(b)
+        turn_queries(0)
+        keep_queries(0, nc.scalar.copy)
+        for b in range(BATCH):
+            x_normalise(b)
+            x_turn(b)
+            if b < 2:
+                x_regroup(b, nc.scalar.copy)
+        nc.scalar.activation(out=warm[:, 1:2], in_=eps_sb[:], func=ACT.Sigmoid)
+        x_quantise(0)
+        x_quantise(1)
+        for b in range(2, BATCH):
+            x_regroup(b, nc.vector.tensor_copy)
+            x_quantise(b)
+        for c in range(BANKS):
+            cols = slice(BANK * c, BANK * (c + 1))
+            nc.gpsimd.tensor_scalar(
+                out=w_sorted[:, cols].rearrange("p (u q e) -> p u q e", u=2, e=2),
+                in0=vw_raw[:, cols].rearrange("p (q u e) -> p u q e", u=2, e=2),
+                scalar1=1.0,
+                scalar2=1.0,
+                op0=ALU.mult,
+                op1=ALU.mult,
+            )
 
         work = ctx.enter_context(tc.tile_pool(name="work", bufs=3))
         out_tiles = out.rearrange("b (i p) d -> (b i) p d", p=P)
@@ -243,7 +306,7 @@ def tile_glamemoryreader_pb_k_kernel(
             nc.tensor.matmul(
                 out=r_bank[:].rearrange("t (u p e) -> t p u e", u=2, e=2),
                 lhsT=q_t[:, u, :],
-                rhs=state[bh][:, BANK * c : BANK * (c + 1)].rearrange("k (p u e) -> k p u e", u=2, e=2),
+                rhs=states[bh][:, BANK * c : BANK * (c + 1)].rearrange("k (p u e) -> k p u e", u=2, e=2),
                 start=True,
                 stop=True,
             )
@@ -273,20 +336,24 @@ def tile_glamemoryreader_pb_k_kernel(
         def partial(u):
             if not exists(u):
                 return
+            terms = BANKS + 1 if u < POW_UNITS else BANKS
             bias = work.tile([P, 1], F32, tag="bias", bufs=4)
-            nc.vector.tensor_reduce(out=bias[:], in_=sums[:, u, 0:BANKS], axis=AXIS.X, op=ALU.add)
+            nc.vector.tensor_reduce(out=bias[:], in_=sums[:, u, 0:terms], axis=AXIS.X, op=ALU.add)
             biases[u] = bias
 
         def root(u):
             if not exists(u):
                 return
             rstd = work.tile([P, 1], F32, tag="rstd", bufs=4)
-            nc.scalar.activation(
-                out=rstd[:],
-                in_=sums[:, u, BANKS : BANKS + 1],
-                func=ACT.Abs_reciprocal_sqrt,
-                bias=biases[u][:, 0:1],
-            )
+            if u < POW_UNITS:
+                nc.gpsimd.tensor_tensor(out=rstd[:], in0=biases[u][:], in1=minus_half[:], op=ALU.pow)
+            else:
+                nc.scalar.activation(
+                    out=rstd[:],
+                    in_=sums[:, u, BANKS : BANKS + 1],
+                    func=ACT.Abs_reciprocal_sqrt,
+                    bias=biases[u][:, 0:1],
+                )
             rstds[u] = rstd
 
         def normalise(u):
@@ -311,7 +378,7 @@ def tile_glamemoryreader_pb_k_kernel(
                 turned[(u, m)] = rt
 
         def regroup(u, copy, first, last):
-            if not exists(u):
+            if not exists(u) or first > last:
                 return
             if first == 0:
                 grouped = work.tile([P, BANKS, P, 4], BF16, tag="grouped", align_bytes=64)
@@ -360,25 +427,42 @@ def tile_glamemoryreader_pb_k_kernel(
             nc.vector.tensor_tensor(out=o_sb[:], in0=accs[i][:], in1=gate_sb[:, i, :], op=ALU.mult)
             nc.sync.dma_start(out=out_tiles[i], in_=o_sb[:])
 
-        for u in range(-1, UNITS + 5):
-            finish(u - 5)
-            for c in range(BANKS // 2):
-                square(u, c + 2)
-                weigh(u, c)
-                read(u + 1, c)
-                project(u - 4, 2 * c)
-                project(u - 4, 2 * c + 1)
-            partial(u)
-            regroup(u - 2, nc.scalar.copy, 0, 1)
+        def scalar_passes(u):
+            return 0 if u < 3 else 3 + (u % 4 == 1)
+
+        for u in range(-1, UNITS + 4):
+            finish(u - 4)
+            gate(2 * u + 2)
+            gate(2 * u + 3)
+            square(u, 2)
+            weigh(u, 0)
+            read(u + 1, 0)
+            project(u - 3, 0)
+            project(u - 3, 1)
+            weigh(u, 1)
+            read(u + 1, 1)
+            project(u - 3, 2)
+            project(u - 3, 3)
+            turn_queries(u + 2)
+            regroup(u - 2, nc.scalar.copy, 0, min(scalar_passes(u - 2), 2) - 1)
+            regroup(u - 2, nc.scalar.copy, 2, scalar_passes(u - 2) - 1)
+            if scalar_passes(u - 2) == 0:
+                regroup(u - 2, nc.vector.tensor_copy, 0, 1)
+            regroup(u - 2, nc.vector.tensor_copy, max(scalar_passes(u - 2), 2), BANKS - 1)
+            square(u, 3)
+            gate_out(2 * u + 2)
+            gate_out(2 * u + 3)
             weigh(u, 2)
             read(u + 1, 2)
-            root(u)
-            regroup(u - 2, nc.scalar.copy, 2, SCALAR_PASSES - 1)
+            partial(u)
             weigh(u, 3)
             read(u + 1, 3)
+            keep_queries(u + 2, nc.vector.tensor_copy)
             square(u + 1, 0)
+            root(u)
             square(u + 1, 1)
             normalise(u)
-            quantise(u - 3)
-            regroup(u - 2, nc.vector.tensor_copy, SCALAR_PASSES, BANKS - 1)
+            quantise(u - 2)
             transpose(u - 1)
+            if HEADS <= u < 2 * HEADS:
+                load_state(STATE_BUFS + u - HEADS)

@@ -167,7 +167,7 @@ def tile_glamemoryreader_pb_k_kernel(
             for j in range(2):
                 x_sq = keep.tile([P, BANK], BF16, tag="x_sq_%d" % j, bufs=2)
                 x_tile = x_sb[:, 2 * b + j, :]
-                if j == 0 or b >= 2:
+                if j == 0 or b >= 3:
                     nc.scalar.activation(
                         out=x_sq[:],
                         in_=x_tile,
@@ -428,41 +428,37 @@ def tile_glamemoryreader_pb_k_kernel(
             nc.sync.dma_start(out=out_tiles[i], in_=o_sb[:])
 
         def scalar_passes(u):
-            return 0 if u < 3 else 3 + (u % 4 == 1)
+            return 0 if u < 2 else 3 + (u % 4 == 2)
 
-        for u in range(-1, UNITS + 4):
-            finish(u - 4)
+        for u in range(-1, UNITS + 5):
+            finish(u - 5)
             gate(2 * u + 2)
             gate(2 * u + 3)
-            square(u, 2)
-            weigh(u, 0)
-            read(u + 1, 0)
-            project(u - 3, 0)
-            project(u - 3, 1)
-            weigh(u, 1)
-            read(u + 1, 1)
-            project(u - 3, 2)
-            project(u - 3, 3)
+            for c in range(BANKS // 2):
+                square(u, c + 2)
+                weigh(u, c)
+                read(u + 1, c)
+                project(u - 4, 2 * c)
+                project(u - 4, 2 * c + 1)
             turn_queries(u + 2)
-            regroup(u - 2, nc.scalar.copy, 0, min(scalar_passes(u - 2), 2) - 1)
-            regroup(u - 2, nc.scalar.copy, 2, scalar_passes(u - 2) - 1)
-            if scalar_passes(u - 2) == 0:
-                regroup(u - 2, nc.vector.tensor_copy, 0, 1)
-            regroup(u - 2, nc.vector.tensor_copy, max(scalar_passes(u - 2), 2), BANKS - 1)
-            square(u, 3)
+            partial(u)
             gate_out(2 * u + 2)
             gate_out(2 * u + 3)
+            regroup(u - 2, nc.scalar.copy, 0, min(scalar_passes(u - 2), 2) - 1)
             weigh(u, 2)
             read(u + 1, 2)
-            partial(u)
+            root(u)
+            regroup(u - 2, nc.scalar.copy, 2, scalar_passes(u - 2) - 1)
             weigh(u, 3)
             read(u + 1, 3)
             keep_queries(u + 2, nc.vector.tensor_copy)
             square(u + 1, 0)
-            root(u)
             square(u + 1, 1)
             normalise(u)
-            quantise(u - 2)
+            quantise(u - 3)
+            if scalar_passes(u - 2) == 0:
+                regroup(u - 2, nc.vector.tensor_copy, 0, 1)
+            regroup(u - 2, nc.vector.tensor_copy, max(scalar_passes(u - 2), 2), BANKS - 1)
             transpose(u - 1)
             if HEADS <= u < 2 * HEADS:
                 load_state(STATE_BUFS + u - HEADS)

@@ -428,9 +428,45 @@ def tile_glamemoryreader_pb_k_kernel(
             nc.sync.dma_start(out=out_tiles[i], in_=o_sb[:])
 
         def scalar_passes(u):
-            return 0 if u < 2 else 3 + (u % 4 == 2)
+            return 4 if u >= UNITS - 4 else 0 if u < 2 else 3
 
-        for u in range(-1, UNITS + 5):
+        def normalise_pass(u, c, engine):
+            if c == 0:
+                rn = work.tile([P, HEAD_V], BF16, tag="rn")
+                normed[u] = rn
+            cols = slice(BANK * c, BANK * (c + 1))
+            if engine == "vector":
+                nc.vector.tensor_scalar(
+                    out=normed[u][:, cols], in0=weighed[u][:, cols], scalar1=rstds[u][:, 0:1], scalar2=1.0, op0=ALU.mult, op1=ALU.mult
+                )
+            else:
+                nc.scalar.activation(
+                    out=normed[u][:, cols], in_=weighed[u][:, cols], func=ACT.Copy, scale=rstds[u][:, 0:1]
+                )
+
+        def transpose_half(u, m, tag, bufs):
+            words = normed[u][:].bitcast(F32)
+            rt = psum.tile([P, 4, P], F32, tag=tag, bufs=bufs)
+            for j in range(4):
+                nc.tensor.transpose(
+                    out=rt[:, j, :], in_=words[:, P * (4 * m + j) : P * (4 * m + j + 1)], identity=ident_f32[:]
+                )
+            turned[(u, m)] = rt
+
+        def quantise_half(u, m):
+            if m == 0:
+                code = work.tile([P, BANKS, P], U32, tag="code", align_bytes=64)
+                plane = work.tile([P, BANKS, P], U8, tag="plane", align_bytes=64)
+                codes[u] = code
+                planes[u] = plane
+            two = slice(2 * m, 2 * m + 2)
+            nc.vector.quantize_mx(
+                out=codes[u][:, two, :].rearrange("p c t -> p (c t)").bitcast(FP8X4),
+                scales=planes[u][:, two, :].rearrange("p c t -> p (c t)"),
+                in_=groups[u][:, two, :, :].rearrange("p c t w -> p (c t w)"),
+            )
+
+        for u in range(-1, UNITS):
             finish(u - 5)
             gate(2 * u + 2)
             gate(2 * u + 3)
@@ -442,6 +478,9 @@ def tile_glamemoryreader_pb_k_kernel(
                 project(u - 4, 2 * c + 1)
             turn_queries(u + 2)
             partial(u)
+            if u == UNITS - 1:
+                for c in range(BANKS):
+                    project(u - 3, c)
             gate_out(2 * u + 2)
             gate_out(2 * u + 3)
             regroup(u - 2, nc.scalar.copy, 0, min(scalar_passes(u - 2), 2) - 1)
@@ -454,11 +493,37 @@ def tile_glamemoryreader_pb_k_kernel(
             keep_queries(u + 2, nc.vector.tensor_copy)
             square(u + 1, 0)
             square(u + 1, 1)
-            normalise(u)
-            quantise(u - 3)
+            if u < UNITS - 1:
+                normalise(u)
+                quantise(u - 3)
+            if u >= UNITS - 2:
+                quantise(u - 2)
             if scalar_passes(u - 2) == 0:
                 regroup(u - 2, nc.vector.tensor_copy, 0, 1)
             regroup(u - 2, nc.vector.tensor_copy, max(scalar_passes(u - 2), 2), BANKS - 1)
             transpose(u - 1)
             if HEADS <= u < 2 * HEADS:
                 load_state(STATE_BUFS + u - HEADS)
+        last = UNITS - 1
+        sc, ve = nc.scalar.copy, nc.vector.tensor_copy
+        normalise_pass(last, 0, "scalar")
+        normalise_pass(last, 1, "scalar")
+        normalise_pass(last, 2, "vector")
+        normalise_pass(last, 3, "vector")
+        transpose_half(last, 0, "read", READ_BANKS)
+        transpose_half(last, 1, "read", READ_BANKS)
+        for c in range(BANKS):
+            project(last - 2, c)
+        regroup(last - 1, sc, 0, 1)
+        regroup(last - 1, ve, 2, 3)
+        quantise(last - 1)
+        regroup(last, sc, 0, 1)
+        regroup(last, ve, 2, 3)
+        for c in range(BANKS):
+            project(last - 1, c)
+        quantise_half(last, 0)
+        quantise_half(last, 1)
+        finish(last - 4)
+        for c in range(BANKS):
+            project(last, c)
+        finish(last)

@@ -55,6 +55,10 @@ def tile_glamemoryreader_pb_k_kernel(
         make_identity(nc, ident_bf16[:])
         ident_f32 = keep.tile([P, P], F32)
         make_identity(nc, ident_f32[:])
+        rows = keep.tile([P, HEAD_V + D_MODEL], BF16)
+        nc.vector.memset(rows[:].bitcast(I32), 0)
+        ones = keep.tile([P, P], BF16)
+        nc.vector.memset(ones[:], 1.0)
         eps_sb = keep.tile([P, 1], F32)
         nc.vector.memset(eps_sb[:], EPS)
         minus_half = keep.tile([P, 1], F32)
@@ -71,10 +75,6 @@ def tile_glamemoryreader_pb_k_kernel(
             keep.tile([P, BANKS, D_MODEL], U32, name="ow_words_%d" % h, align_bytes=64) for h in range(HEADS)
         ]
 
-        ones = keep.tile([P, P], BF16)
-        nc.vector.memset(ones[:], 1.0)
-        nw_row = keep.tile([P, D_MODEL], BF16)
-        nc.vector.memset(nw_row[:].bitcast(I32), 0)
         nc.vector.memset(ow_planes[:].bitcast(I32), 0)
         nc.vector.memset(sums[:], EPS)
 
@@ -83,7 +83,6 @@ def tile_glamemoryreader_pb_k_kernel(
         q_sb = keep.tile([P, TOKEN_TILES, HEADS * P], BF16)
         q_dram = q_hat.rearrange("b (i p) h k -> p (b i) (h k)", p=P)
         gw_words = keep.tile([P, D_MODEL], U32, align_bytes=64)
-        vw_raw = keep.tile([P, HEAD_V], BF16)
 
         states = {}
 
@@ -99,12 +98,12 @@ def tile_glamemoryreader_pb_k_kernel(
             nc.sync.dma_start(out=q_sb[:, 2 * first : 2 * last + 2, :], in_=q_dram[:, 2 * first : 2 * last + 2, :])
 
         load_x(0)
-        nc.sync.dma_start(out=nw_row[0:1, :], in_=norm_w.unsqueeze(0))
+        nc.sync.dma_start(out=rows[0:1, 0:HEAD_V], in_=v_norm_w.unsqueeze(0))
+        nc.sync.dma_start(out=rows[0:1, HEAD_V:], in_=norm_w.unsqueeze(0))
         for b in range(1, BATCH):
             load_x(b)
         load_q(0, 0)
         load_state(0)
-        nc.sync.dma_start(out=vw_raw[:], in_=v_norm_w.partition_broadcast(P))
         nc.sync.dma_start(
             out=gw_words[:].bitcast(I32),
             in_=gate_w_words[0].rearrange("p n t -> p (n t)").bitcast(I32),
@@ -147,7 +146,21 @@ def tile_glamemoryreader_pb_k_kernel(
                 copy(out=q_t[:, 2 * HEADS * b : 2 * HEADS * (b + 1), :], in_=q_turned[b][:])
 
         nw_ps = psum.tile([P, D_MODEL], F32, tag="acc", bufs=2)
-        nc.tensor.matmul(out=nw_ps[:], lhsT=ones[:], rhs=nw_row[:], start=True, stop=True)
+        nc.tensor.matmul(out=nw_ps[:], lhsT=ones[:], rhs=rows[:, HEAD_V:], start=True, stop=True)
+        w_banks = []
+        for c in range(BANKS):
+            w_ps = psum.tile([P, BANK], F32, tag="read", bufs=READ_BANKS)
+            nc.tensor.matmul(
+                out=w_ps[:].rearrange("t (u p e) -> t p u e", u=2, e=2),
+                lhsT=ones[:],
+                rhs=rows[:, BANK * c : BANK * (c + 1)].rearrange("k (p u e) -> k p u e", u=2, e=2),
+                start=True,
+                stop=True,
+            )
+            w_banks.append(w_ps)
+
+        def keep_weights(c, copy):
+            copy(out=w_sorted[:, BANK * c : BANK * (c + 1)], in_=w_banks[c][:])
 
         warm = keep.tile([P, 2], F32)
         nc.scalar.activation(out=warm[:, 0:1], in_=eps_sb[:], func=ACT.Abs_reciprocal_sqrt)
@@ -258,6 +271,10 @@ def tile_glamemoryreader_pb_k_kernel(
 
         for b in range(BATCH):
             x_stats(b)
+        keep_weights(0, nc.scalar.copy)
+        keep_weights(1, nc.scalar.copy)
+        keep_weights(2, nc.vector.tensor_copy)
+        keep_weights(3, nc.vector.tensor_copy)
         turn_queries(0)
         keep_queries(0, nc.scalar.copy)
         for b in range(BATCH):
@@ -271,16 +288,6 @@ def tile_glamemoryreader_pb_k_kernel(
         for b in range(2, BATCH):
             x_regroup(b, nc.vector.tensor_copy)
             x_quantise(b)
-        for c in range(BANKS):
-            cols = slice(BANK * c, BANK * (c + 1))
-            nc.gpsimd.tensor_scalar(
-                out=w_sorted[:, cols].rearrange("p (u q e) -> p u q e", u=2, e=2),
-                in0=vw_raw[:, cols].rearrange("p (q u e) -> p u q e", u=2, e=2),
-                scalar1=1.0,
-                scalar2=1.0,
-                op0=ALU.mult,
-                op1=ALU.mult,
-            )
 
         work = ctx.enter_context(tc.tile_pool(name="work", bufs=3))
         out_tiles = out.rearrange("b (i p) d -> (b i) p d", p=P)

@@ -55,8 +55,10 @@ def tile_glamemoryreader_pb_k_kernel(
         make_identity(nc, ident_bf16[:])
         ident_f32 = keep.tile([P, P], F32)
         make_identity(nc, ident_f32[:])
-        rows = keep.tile([P, HEAD_V + D_MODEL], BF16)
-        nc.vector.memset(rows[:].bitcast(I32), 0)
+        nw_row = keep.tile([P, D_MODEL], BF16)
+        nc.vector.memset(nw_row[:].bitcast(I32), 0)
+        vw_row = keep.tile([P, HEAD_V], BF16)
+        nc.vector.memset(vw_row[:].bitcast(I32), 0)
         ones = keep.tile([P, P], BF16)
         nc.vector.memset(ones[:], 1.0)
         eps_sb = keep.tile([P, 1], F32)
@@ -98,10 +100,11 @@ def tile_glamemoryreader_pb_k_kernel(
             nc.sync.dma_start(out=q_sb[:, 2 * first : 2 * last + 2, :], in_=q_dram[:, 2 * first : 2 * last + 2, :])
 
         load_x(0)
-        nc.sync.dma_start(out=rows[0:1, 0:HEAD_V], in_=v_norm_w.unsqueeze(0))
-        nc.sync.dma_start(out=rows[0:1, HEAD_V:], in_=norm_w.unsqueeze(0))
-        for b in range(1, BATCH):
-            load_x(b)
+        nc.sync.dma_start(out=nw_row[0:1, :], in_=norm_w.unsqueeze(0))
+        load_x(1)
+        load_x(2)
+        load_x(3)
+        nc.sync.dma_start(out=vw_row[0:1, :], in_=v_norm_w.unsqueeze(0))
         load_q(0, 0)
         load_state(0)
         nc.sync.dma_start(
@@ -146,21 +149,25 @@ def tile_glamemoryreader_pb_k_kernel(
                 copy(out=q_t[:, 2 * HEADS * b : 2 * HEADS * (b + 1), :], in_=q_turned[b][:])
 
         nw_ps = psum.tile([P, D_MODEL], F32, tag="acc", bufs=2)
-        nc.tensor.matmul(out=nw_ps[:], lhsT=ones[:], rhs=rows[:, HEAD_V:], start=True, stop=True)
+        nc.tensor.matmul(out=nw_ps[:], lhsT=ones[:], rhs=nw_row[:], start=True, stop=True)
         w_banks = []
-        for c in range(BANKS):
-            w_ps = psum.tile([P, BANK], F32, tag="read", bufs=READ_BANKS)
-            nc.tensor.matmul(
-                out=w_ps[:].rearrange("t (u p e) -> t p u e", u=2, e=2),
-                lhsT=ones[:],
-                rhs=rows[:, BANK * c : BANK * (c + 1)].rearrange("k (p u e) -> k p u e", u=2, e=2),
-                start=True,
-                stop=True,
-            )
+        for m in range(BANKS // 2):
+            w_ps = psum.tile([P, 2, BANK], BF16, tag="read", bufs=READ_BANKS)
+            for j in range(2):
+                c = 2 * m + j
+                nc.tensor.matmul(
+                    out=w_ps[:, j, :].rearrange("t (u p e) -> t p u e", u=2, e=2),
+                    lhsT=ones[:],
+                    rhs=vw_row[:, BANK * c : BANK * (c + 1)].rearrange("k (p u e) -> k p u e", u=2, e=2),
+                    start=True,
+                    stop=True,
+                )
             w_banks.append(w_ps)
 
-        def keep_weights(c, copy):
-            copy(out=w_sorted[:, BANK * c : BANK * (c + 1)], in_=w_banks[c][:])
+        def keep_weights(m, copy):
+            copy(
+                out=w_sorted[:, 2 * BANK * m : 2 * BANK * (m + 1)], in_=w_banks[m][:].rearrange("p j k -> p (j k)")
+            )
 
         warm = keep.tile([P, 2], F32)
         nc.scalar.activation(out=warm[:, 0:1], in_=eps_sb[:], func=ACT.Abs_reciprocal_sqrt)
@@ -180,7 +187,7 @@ def tile_glamemoryreader_pb_k_kernel(
             for j in range(2):
                 x_sq = keep.tile([P, BANK], BF16, tag="x_sq_%d" % j, bufs=2)
                 x_tile = x_sb[:, 2 * b + j, :]
-                if j == 0 or b >= 3:
+                if j == 0 or b >= 4:
                     nc.scalar.activation(
                         out=x_sq[:],
                         in_=x_tile,
@@ -269,15 +276,15 @@ def tile_glamemoryreader_pb_k_kernel(
             if 0 <= i < TOKEN_TILES:
                 nc.scalar.activation(out=gate_sb[:, i, :], in_=g_accs[i][:], func=ACT.Sigmoid)
 
-        for b in range(BATCH):
-            x_stats(b)
+        x_stats(0)
+        x_stats(1)
+        x_stats(2)
+        x_stats(3)
         keep_weights(0, nc.scalar.copy)
         keep_weights(1, nc.scalar.copy)
-        keep_weights(2, nc.vector.tensor_copy)
-        keep_weights(3, nc.vector.tensor_copy)
         turn_queries(0)
         keep_queries(0, nc.scalar.copy)
-        for b in range(BATCH):
+        for b in range(4):
             x_normalise(b)
             x_turn(b)
             if b < 2:
@@ -285,9 +292,10 @@ def tile_glamemoryreader_pb_k_kernel(
         nc.scalar.activation(out=warm[:, 1:2], in_=eps_sb[:], func=ACT.Sigmoid)
         x_quantise(0)
         x_quantise(1)
-        for b in range(2, BATCH):
-            x_regroup(b, nc.vector.tensor_copy)
-            x_quantise(b)
+        x_regroup(2, nc.vector.tensor_copy)
+        x_quantise(2)
+        x_regroup(3, nc.vector.tensor_copy)
+        x_quantise(3)
 
         work = ctx.enter_context(tc.tile_pool(name="work", bufs=3))
         out_tiles = out.rearrange("b (i p) d -> (b i) p d", p=P)
@@ -426,13 +434,15 @@ def tile_glamemoryreader_pb_k_kernel(
                 stop=(h == HEADS - 1 and c == BANKS - 1),
             )
 
-        def finish(u):
+        def finish(u, parts=1):
             if not exists(u) or u % HEADS != HEADS - 1:
                 return
             i = u // HEADS
             o_sb = work.tile([P, D_MODEL], F32, tag="o_sb", bufs=2)
-            nc.vector.tensor_tensor(out=o_sb[:], in0=accs[i][:], in1=gate_sb[:, i, :], op=ALU.mult)
-            nc.sync.dma_start(out=out_tiles[i], in_=o_sb[:])
+            for part in range(parts):
+                cols = slice(D_MODEL // parts * part, D_MODEL // parts * (part + 1))
+                nc.vector.tensor_tensor(out=o_sb[:, cols], in0=accs[i][:, cols], in1=gate_sb[:, i, cols], op=ALU.mult)
+                nc.sync.dma_start(out=out_tiles[i][:, cols], in_=o_sb[:, cols])
 
         def scalar_passes(u):
             return 4 if u >= UNITS - 4 else 0 if u < 2 else 3
@@ -517,13 +527,13 @@ def tile_glamemoryreader_pb_k_kernel(
         normalise_pass(last, 1, "scalar")
         normalise_pass(last, 2, "vector")
         normalise_pass(last, 3, "vector")
+        regroup(last - 1, sc, 0, 1)
+        regroup(last - 1, ve, 2, 3)
+        quantise(last - 1)
         transpose_half(last, 0, "read", READ_BANKS)
         transpose_half(last, 1, "read", READ_BANKS)
         for c in range(BANKS):
             project(last - 2, c)
-        regroup(last - 1, sc, 0, 1)
-        regroup(last - 1, ve, 2, 3)
-        quantise(last - 1)
         regroup(last, sc, 0, 1)
         regroup(last, ve, 2, 3)
         for c in range(BANKS):
@@ -533,4 +543,4 @@ def tile_glamemoryreader_pb_k_kernel(
         finish(last - 4)
         for c in range(BANKS):
             project(last, c)
-        finish(last)
+        finish(last, 2)

@@ -19,17 +19,23 @@ SEQ = 256
 D_MODEL = 512
 HEADS = 4
 HEAD_V = 2048
-TOKEN_TILES = BATCH * SEQ // P
 TILES_PER_BATCH = SEQ // P
+TOKEN_TILES = BATCH * TILES_PER_BATCH
 BANK = 512
 BANKS = HEAD_V // BANK
 UNITS = TOKEN_TILES * HEADS
+LAST = UNITS - 1
 STATE_BUFS = 12
-POW_UNITS = 3
 READ_BANKS = 4
-SCALAR_PASSES = 3
+POW_UNITS = 3
 EPS = 1e-5
 FLOPS = 2 * (1024 * 8192 * 512 + 1024 * 512 * 512 + 16 * 256 * 128 * 2048)
+
+
+def scalar_passes(u):
+    if u < 2:
+        return 0
+    return 3 if u < UNITS - 4 else 4
 
 
 def tile_glamemoryreader_pb_k_kernel(
@@ -48,6 +54,7 @@ def tile_glamemoryreader_pb_k_kernel(
     nc = tc.nc
     with ExitStack() as ctx:
         keep = ctx.enter_context(tc.tile_pool(name="keep", bufs=1))
+        work = ctx.enter_context(tc.tile_pool(name="work", bufs=3))
         psum = ctx.enter_context(tc.psum_pool(name="psum", bufs=1))
         ctx.enter_context(tc.manual_schedule())
 
@@ -55,10 +62,10 @@ def tile_glamemoryreader_pb_k_kernel(
         make_identity(nc, ident_bf16[:])
         ident_f32 = keep.tile([P, P], F32)
         make_identity(nc, ident_f32[:])
-        nw_row = keep.tile([P, D_MODEL], BF16)
-        nc.vector.memset(nw_row[:].bitcast(I32), 0)
-        vw_row = keep.tile([P, HEAD_V], BF16)
-        nc.vector.memset(vw_row[:].bitcast(I32), 0)
+        norm_row = keep.tile([P, D_MODEL], BF16)
+        nc.vector.memset(norm_row[:].bitcast(I32), 0)
+        v_norm_row = keep.tile([P, HEAD_V], BF16)
+        nc.vector.memset(v_norm_row[:].bitcast(I32), 0)
         ones = keep.tile([P, P], BF16)
         nc.vector.memset(ones[:], 1.0)
         eps_sb = keep.tile([P, 1], F32)
@@ -68,53 +75,53 @@ def tile_glamemoryreader_pb_k_kernel(
         gw_planes = keep.tile([P, D_MODEL], U8, align_bytes=64)
         nc.vector.memset(gw_planes[:].bitcast(I32), 0)
         ow_planes = keep.tile([P, HEADS * BANKS, D_MODEL], U8, align_bytes=64)
+        nc.vector.memset(ow_planes[:].bitcast(I32), 0)
         sums = keep.tile([P, UNITS, 8], F32)
+        nc.vector.memset(sums[:], EPS)
 
         gate_sb = keep.tile([P, TOKEN_TILES, D_MODEL], F32)
         q_t = keep.tile([P, UNITS, P], BF16)
         w_sorted = keep.tile([P, HEAD_V], BF16)
+        x_sb = keep.tile([P, TOKEN_TILES, D_MODEL], BF16)
+        q_sb = keep.tile([P, TOKEN_TILES, HEADS * P], BF16)
+        gw_words = keep.tile([P, D_MODEL], U32, align_bytes=64)
         ow_words = [
             keep.tile([P, BANKS, D_MODEL], U32, name="ow_words_%d" % h, align_bytes=64) for h in range(HEADS)
         ]
+        x_rstd = keep.tile([P, TOKEN_TILES], F32)
+        x_codes = keep.tile([P, TOKEN_TILES, P], U32, align_bytes=64)
+        x_planes = keep.tile([P, TOKEN_TILES, P], U8, align_bytes=64)
 
-        nc.vector.memset(ow_planes[:].bitcast(I32), 0)
-        nc.vector.memset(sums[:], EPS)
-
-        x_sb = keep.tile([P, TOKEN_TILES, D_MODEL], BF16)
         x_dram = hidden_states.rearrange("b (i p) d -> p (b i) d", p=P)
-        q_sb = keep.tile([P, TOKEN_TILES, HEADS * P], BF16)
         q_dram = q_hat.rearrange("b (i p) h k -> p (b i) (h k)", p=P)
-        gw_words = keep.tile([P, D_MODEL], U32, align_bytes=64)
-
+        out_tiles = out.rearrange("b (i p) d -> (b i) p d", p=P)
         states = {}
+
+        def pair(b):
+            return slice(TILES_PER_BATCH * b, TILES_PER_BATCH * (b + 1))
+
+        def load_x(b):
+            nc.sync.dma_start(out=x_sb[:, pair(b), :], in_=x_dram[:, pair(b), :])
 
         def load_state(bh):
             state = keep.tile([P, HEAD_V], BF16, tag="state", bufs=STATE_BUFS)
             nc.sync.dma_start(out=state[:], in_=recurrent_state[bh // HEADS, bh % HEADS])
             states[bh] = state
 
-        def load_x(b):
-            nc.sync.dma_start(out=x_sb[:, 2 * b : 2 * b + 2, :], in_=x_dram[:, 2 * b : 2 * b + 2, :])
-
-        def load_q(first, last):
-            nc.sync.dma_start(out=q_sb[:, 2 * first : 2 * last + 2, :], in_=q_dram[:, 2 * first : 2 * last + 2, :])
-
         load_x(0)
-        nc.sync.dma_start(out=nw_row[0:1, :], in_=norm_w.unsqueeze(0))
-        load_x(1)
-        load_x(2)
-        load_x(3)
-        nc.sync.dma_start(out=vw_row[0:1, :], in_=v_norm_w.unsqueeze(0))
-        load_q(0, 0)
+        nc.sync.dma_start(out=norm_row[0:1, :], in_=norm_w.unsqueeze(0))
+        for b in range(1, BATCH):
+            load_x(b)
+        nc.sync.dma_start(out=v_norm_row[0:1, :], in_=v_norm_w.unsqueeze(0))
+        nc.sync.dma_start(out=q_sb[:, pair(0), :], in_=q_dram[:, pair(0), :])
         load_state(0)
         nc.sync.dma_start(
-            out=gw_words[:].bitcast(I32),
-            in_=gate_w_words[0].rearrange("p n t -> p (n t)").bitcast(I32),
+            out=gw_words[:].bitcast(I32), in_=gate_w_words[0].rearrange("p n t -> p (n t)").bitcast(I32)
         )
         for r in range(4):
             nc.sync.dma_start(out=gw_planes[r:P:32, :].bitcast(I32), in_=gate_w_scales[0, r:16:4, :].bitcast(I32))
         load_state(1)
-        load_q(1, BATCH - 1)
+        nc.sync.dma_start(out=q_sb[:, TILES_PER_BATCH:, :], in_=q_dram[:, TILES_PER_BATCH:, :])
         load_state(2)
         load_state(3)
         for r in range(4):
@@ -130,64 +137,53 @@ def tile_glamemoryreader_pb_k_kernel(
         for bh in range(HEADS, STATE_BUFS):
             load_state(bh)
 
+        norm_ps = psum.tile([P, D_MODEL], F32, tag="acc", bufs=2)
+        nc.tensor.matmul(out=norm_ps[:], lhsT=ones[:], rhs=norm_row[:], start=True, stop=True)
+        v_norm_ps = []
+        for m in range(BANKS // 2):
+            two_passes = psum.tile([P, 2, BANK], BF16, tag="read", bufs=READ_BANKS)
+            for j in range(2):
+                c = 2 * m + j
+                nc.tensor.matmul(
+                    out=two_passes[:, j, :].rearrange("t (s p e) -> t p s e", s=2, e=2),
+                    lhsT=ones[:],
+                    rhs=v_norm_row[:, BANK * c : BANK * (c + 1)].rearrange("k (p s e) -> k p s e", s=2, e=2),
+                    start=True,
+                    stop=True,
+                )
+            v_norm_ps.append(two_passes)
+
         q_turned = {}
 
         def turn_queries(b):
-            if not 0 <= b < BATCH:
+            if b >= BATCH:
                 return
-            qt_ps = psum.tile([P, 2 * HEADS, P], BF16, tag="turn", bufs=2)
-            for j in range(2 * HEADS):
+            qt_ps = psum.tile([P, TILES_PER_BATCH * HEADS, P], BF16, tag="turn", bufs=2)
+            for j in range(TILES_PER_BATCH * HEADS):
+                h = j % HEADS
                 nc.tensor.transpose(
                     out=qt_ps[:, j, :],
-                    in_=q_sb[:, 2 * b + j // HEADS, P * (j % HEADS) : P * (j % HEADS + 1)],
+                    in_=q_sb[:, TILES_PER_BATCH * b + j // HEADS, P * h : P * (h + 1)],
                     identity=ident_bf16[:],
                 )
             q_turned[b] = qt_ps
 
         def keep_queries(b, copy):
-            if 0 <= b < BATCH:
-                copy(out=q_t[:, 2 * HEADS * b : 2 * HEADS * (b + 1), :], in_=q_turned[b][:])
+            if b < BATCH:
+                units = slice(TILES_PER_BATCH * HEADS * b, TILES_PER_BATCH * HEADS * (b + 1))
+                copy(out=q_t[:, units, :], in_=q_turned[b][:])
 
-        nw_ps = psum.tile([P, D_MODEL], F32, tag="acc", bufs=2)
-        nc.tensor.matmul(out=nw_ps[:], lhsT=ones[:], rhs=nw_row[:], start=True, stop=True)
-        w_banks = []
-        for m in range(BANKS // 2):
-            w_ps = psum.tile([P, 2, BANK], BF16, tag="read", bufs=READ_BANKS)
-            for j in range(2):
-                c = 2 * m + j
-                nc.tensor.matmul(
-                    out=w_ps[:, j, :].rearrange("t (u p e) -> t p u e", u=2, e=2),
-                    lhsT=ones[:],
-                    rhs=vw_row[:, BANK * c : BANK * (c + 1)].rearrange("k (p u e) -> k p u e", u=2, e=2),
-                    start=True,
-                    stop=True,
-                )
-            w_banks.append(w_ps)
-
-        def keep_weights(m, copy):
-            copy(
-                out=w_sorted[:, 2 * BANK * m : 2 * BANK * (m + 1)], in_=w_banks[m][:].rearrange("p j k -> p (j k)")
-            )
-
-        warm = keep.tile([P, 2], F32)
-        nc.scalar.activation(out=warm[:, 0:1], in_=eps_sb[:], func=ACT.Abs_reciprocal_sqrt)
-        x_rstd = keep.tile([P, TOKEN_TILES], F32)
         x_normed = {}
-        x_grouped = {}
-        x_codes = keep.tile([P, TOKEN_TILES, P], U32, align_bytes=64)
-        x_scales = keep.tile([P, TOKEN_TILES, P], U8, align_bytes=64)
         x_turned = {}
+        x_grouped = {}
+        gate_ps = {}
 
-        def is_pair(b):
-            return 0 <= b < BATCH
-
-        def x_stats(b):
-            two = slice(2 * b, 2 * b + 2)
-            x_ms = keep.tile([P, 2], F32, tag="x_ms_%d" % b, bufs=1)
-            for j in range(2):
-                x_sq = keep.tile([P, BANK], BF16, tag="x_sq_%d" % j, bufs=2)
-                x_tile = x_sb[:, 2 * b + j, :]
-                if j == 0 or b >= 4:
+        def x_root(b):
+            x_ms = keep.tile([P, TILES_PER_BATCH], F32, tag="x_ms", bufs=BATCH)
+            for j in range(TILES_PER_BATCH):
+                x_sq = keep.tile([P, D_MODEL], BF16, tag="x_sq_%d" % j, bufs=2)
+                x_tile = x_sb[:, TILES_PER_BATCH * b + j, :]
+                if j == 0:
                     nc.scalar.activation(
                         out=x_sq[:],
                         in_=x_tile,
@@ -206,101 +202,67 @@ def tile_glamemoryreader_pb_k_kernel(
                         accum_out=x_ms[:, j : j + 1],
                     )
             nc.scalar.activation(
-                out=x_rstd[:, two], in_=x_ms[:], func=ACT.Abs_reciprocal_sqrt, bias=eps_sb[:, 0:1]
+                out=x_rstd[:, pair(b)], in_=x_ms[:], func=ACT.Abs_reciprocal_sqrt, bias=eps_sb[:, 0:1]
             )
 
         def x_normalise(b):
-            if not is_pair(b):
-                return
-            xn = keep.tile([P, 2, D_MODEL], BF16, tag="xn", bufs=2)
-            for j in range(2):
-                i = 2 * b + j
+            xn = keep.tile([P, TILES_PER_BATCH, D_MODEL], BF16, tag="xn", bufs=2)
+            for j in range(TILES_PER_BATCH):
+                i = TILES_PER_BATCH * b + j
                 nc.vector.scalar_tensor_tensor(
                     out=xn[:, j, :],
                     in0=x_sb[:, i, :],
                     scalar=x_rstd[:, i : i + 1],
-                    in1=nw_ps[:],
+                    in1=norm_ps[:],
                     op0=ALU.mult,
                     op1=ALU.mult,
                 )
             x_normed[b] = xn
 
         def x_turn(b):
-            if not is_pair(b):
-                return
-            xt = psum.tile([P, 4, P], F32, tag="turn", bufs=2)
-            for j in range(2):
-                for u in range(2):
+            xt = psum.tile([P, 2 * TILES_PER_BATCH, P], F32, tag="turn", bufs=2)
+            for j in range(TILES_PER_BATCH):
+                for s in range(2):
                     nc.tensor.transpose(
-                        out=xt[:, 2 * j + u, :],
-                        in_=x_normed[b][:, j, :].bitcast(F32)[:, u : D_MODEL // 2 : 2],
+                        out=xt[:, 2 * j + s, :],
+                        in_=x_normed[b][:, j, :].bitcast(F32)[:, s : D_MODEL // 2 : 2],
                         identity=ident_f32[:],
                     )
             x_turned[b] = xt
 
         def x_regroup(b, copy):
-            if not is_pair(b):
-                return
-            xg = keep.tile([P, 2, P, 4], BF16, tag="xg", bufs=2, align_bytes=64)
-            copy(out=xg[:].bitcast(F32), in_=x_turned[b][:].rearrange("p (i u) t -> p i t u", u=2))
+            xg = keep.tile([P, TILES_PER_BATCH, P, 4], BF16, tag="xg", bufs=2, align_bytes=64)
+            copy(out=xg[:].bitcast(F32), in_=x_turned[b][:].rearrange("p (i s) t -> p i t s", s=2))
             x_grouped[b] = xg
 
         def x_quantise(b):
-            if not is_pair(b):
-                return
-            two = slice(2 * b, 2 * b + 2)
             nc.vector.quantize_mx(
-                out=x_codes[:, two, :].rearrange("p i t -> p (i t)").bitcast(FP8X4),
-                scales=x_scales[:, two, :].rearrange("p i t -> p (i t)"),
+                out=x_codes[:, pair(b), :].rearrange("p i t -> p (i t)").bitcast(FP8X4),
+                scales=x_planes[:, pair(b), :].rearrange("p i t -> p (i t)"),
                 in_=x_grouped[b][:].rearrange("p i t w -> p (i t w)"),
             )
 
-        g_accs = {}
-
-        def gate(i):
-            if not 0 <= i < TOKEN_TILES:
+        def multiply_gate(i):
+            if i >= TOKEN_TILES:
                 return
-            g_acc = psum.tile([P, BANK], F32, tag="acc", bufs=2)
+            product = psum.tile([P, D_MODEL], F32, tag="acc", bufs=2)
             nc.tensor.matmul_mx(
-                out=g_acc[:],
+                out=product[:],
                 lhsT=x_codes[:, i, :].bitcast(FP8X4),
-                lhsT_scale=x_scales[:, i, :],
+                lhsT_scale=x_planes[:, i, :],
                 rhs=gw_words[:].bitcast(FP8X4),
                 rhs_scale=gw_planes[:],
                 start=True,
                 stop=True,
             )
-            g_accs[i] = g_acc
+            gate_ps[i] = product
 
-        def gate_out(i):
-            if 0 <= i < TOKEN_TILES:
-                nc.scalar.activation(out=gate_sb[:, i, :], in_=g_accs[i][:], func=ACT.Sigmoid)
+        def open_gate(i):
+            if i < TOKEN_TILES:
+                nc.scalar.activation(out=gate_sb[:, i, :], in_=gate_ps[i][:], func=ACT.Sigmoid)
 
-        x_stats(0)
-        x_stats(1)
-        x_stats(2)
-        x_stats(3)
-        keep_weights(0, nc.scalar.copy)
-        keep_weights(1, nc.scalar.copy)
-        turn_queries(0)
-        keep_queries(0, nc.scalar.copy)
-        for b in range(4):
-            x_normalise(b)
-            x_turn(b)
-            if b < 2:
-                x_regroup(b, nc.scalar.copy)
-        nc.scalar.activation(out=warm[:, 1:2], in_=eps_sb[:], func=ACT.Sigmoid)
-        x_quantise(0)
-        x_quantise(1)
-        x_regroup(2, nc.vector.tensor_copy)
-        x_quantise(2)
-        x_regroup(3, nc.vector.tensor_copy)
-        x_quantise(3)
-
-        work = ctx.enter_context(tc.tile_pool(name="work", bufs=3))
-        out_tiles = out.rearrange("b (i p) d -> (b i) p d", p=P)
         r_banks = {}
-        biases = {}
+        partial_sums = {}
         rstds = {}
         weighed = {}
         normed = {}
@@ -319,9 +281,9 @@ def tile_glamemoryreader_pb_k_kernel(
             r_bank = psum.tile([P, BANK], F32, tag="read", bufs=READ_BANKS)
             bh = HEADS * (u // HEADS // TILES_PER_BATCH) + u % HEADS
             nc.tensor.matmul(
-                out=r_bank[:].rearrange("t (u p e) -> t p u e", u=2, e=2),
+                out=r_bank[:].rearrange("t (s p e) -> t p s e", s=2, e=2),
                 lhsT=q_t[:, u, :],
-                rhs=states[bh][:, BANK * c : BANK * (c + 1)].rearrange("k (p u e) -> k p u e", u=2, e=2),
+                rhs=states[bh][:, BANK * c : BANK * (c + 1)].rearrange("k (p s e) -> k p s e", s=2, e=2),
                 start=True,
                 stop=True,
             )
@@ -348,27 +310,28 @@ def tile_glamemoryreader_pb_k_kernel(
             cols = slice(BANK * c, BANK * (c + 1))
             nc.vector.tensor_tensor(out=weighed[u][:, cols], in0=r_banks[(u, c)][:], in1=w_sorted[:, cols], op=ALU.mult)
 
-        def partial(u):
+        def add_squares(u, banks):
             if not exists(u):
                 return
-            terms = BANKS + 1 if u < POW_UNITS else BANKS
-            bias = work.tile([P, 1], F32, tag="bias", bufs=4)
-            nc.vector.tensor_reduce(out=bias[:], in_=sums[:, u, 0:terms], axis=AXIS.X, op=ALU.add)
-            biases[u] = bias
+            partial = work.tile([P, 1], F32, tag="partial", bufs=4)
+            nc.vector.tensor_reduce(out=partial[:], in_=sums[:, u, 0 : banks + 1], axis=AXIS.X, op=ALU.add)
+            partial_sums[u] = partial
 
-        def root(u):
+        def root_by_pow(u):
             if not exists(u):
                 return
             rstd = work.tile([P, 1], F32, tag="rstd", bufs=4)
-            if u < POW_UNITS:
-                nc.gpsimd.tensor_tensor(out=rstd[:], in0=biases[u][:], in1=minus_half[:], op=ALU.pow)
-            else:
-                nc.scalar.activation(
-                    out=rstd[:],
-                    in_=sums[:, u, BANKS : BANKS + 1],
-                    func=ACT.Abs_reciprocal_sqrt,
-                    bias=biases[u][:, 0:1],
-                )
+            nc.gpsimd.tensor_tensor(out=rstd[:], in0=partial_sums[u][:], in1=minus_half[:], op=ALU.pow)
+            rstds[u] = rstd
+
+        def root(u):
+            rstd = work.tile([P, 1], F32, tag="rstd", bufs=4)
+            nc.scalar.activation(
+                out=rstd[:],
+                in_=sums[:, u, BANKS : BANKS + 1],
+                func=ACT.Abs_reciprocal_sqrt,
+                bias=partial_sums[u][:, 0:1],
+            )
             rstds[u] = rstd
 
         def normalise(u):
@@ -380,59 +343,61 @@ def tile_glamemoryreader_pb_k_kernel(
             )
             normed[u] = rn
 
-        def transpose(u):
+        def transpose(u, tag, bufs):
             if not exists(u):
                 return
             words = normed[u][:].bitcast(F32)
-            for m in range(2):
-                rt = psum.tile([P, 4, P], F32, tag="turn", bufs=2)
+            for m in range(BANKS // 2):
+                rt = psum.tile([P, 4, P], F32, tag=tag, bufs=bufs)
                 for j in range(4):
                     nc.tensor.transpose(
                         out=rt[:, j, :], in_=words[:, P * (4 * m + j) : P * (4 * m + j + 1)], identity=ident_f32[:]
                     )
                 turned[(u, m)] = rt
 
-        def regroup(u, copy, first, last):
-            if not exists(u) or first > last:
+        def regroup(u, copy, first, end):
+            if not exists(u) or first >= end:
                 return
             if first == 0:
                 grouped = work.tile([P, BANKS, P, 4], BF16, tag="grouped", align_bytes=64)
                 groups[u] = grouped
-            bank = turned[(u, first // 2)]
+            m = first // 2
             copy(
-                out=groups[u][:, first : last + 1, :, :].bitcast(F32),
-                in_=bank[:, 2 * (first % 2) : 2 * (last % 2) + 2, :].rearrange("p (c u) t -> p c t u", u=2),
+                out=groups[u][:, first:end, :, :].bitcast(F32),
+                in_=turned[(u, m)][:, 2 * first - 4 * m : 2 * end - 4 * m, :].rearrange("p (c s) t -> p c t s", s=2),
             )
 
-        def quantise(u):
+        def quantise(u, first=0, end=BANKS):
             if not exists(u):
                 return
-            code = work.tile([P, BANKS, P], U32, tag="code", align_bytes=64)
-            plane = work.tile([P, BANKS, P], U8, tag="plane", align_bytes=64)
+            if first == 0:
+                code = work.tile([P, BANKS, P], U32, tag="code", align_bytes=64)
+                plane = work.tile([P, BANKS, P], U8, tag="plane", align_bytes=64)
+                codes[u] = code
+                planes[u] = plane
             nc.vector.quantize_mx(
-                out=code[:].rearrange("p c t -> p (c t)").bitcast(FP8X4),
-                scales=plane[:].rearrange("p c t -> p (c t)"),
-                in_=groups[u][:].rearrange("p c t w -> p (c t w)"),
+                out=codes[u][:, first:end, :].rearrange("p c t -> p (c t)").bitcast(FP8X4),
+                scales=planes[u][:, first:end, :].rearrange("p c t -> p (c t)"),
+                in_=groups[u][:, first:end, :, :].rearrange("p c t w -> p (c t w)"),
             )
-            codes[u] = code
-            planes[u] = plane
 
-        def project(u, c):
+        def project(u, first=0, end=BANKS):
             if not exists(u):
                 return
             h = u % HEADS
-            if h == 0 and c == 0:
-                acc = psum.tile([P, BANK], F32, tag="acc", bufs=2)
-                accs[u // HEADS] = acc
-            nc.tensor.matmul_mx(
-                out=accs[u // HEADS][:],
-                lhsT=codes[u][:, c, :].bitcast(FP8X4),
-                lhsT_scale=planes[u][:, c, :],
-                rhs=ow_words[h][:, c, :].bitcast(FP8X4),
-                rhs_scale=ow_planes[:, BANKS * h + c, :],
-                start=(h == 0 and c == 0),
-                stop=(h == HEADS - 1 and c == BANKS - 1),
-            )
+            for c in range(first, end):
+                if h == 0 and c == 0:
+                    acc = psum.tile([P, D_MODEL], F32, tag="acc", bufs=2)
+                    accs[u // HEADS] = acc
+                nc.tensor.matmul_mx(
+                    out=accs[u // HEADS][:],
+                    lhsT=codes[u][:, c, :].bitcast(FP8X4),
+                    lhsT_scale=planes[u][:, c, :],
+                    rhs=ow_words[h][:, c, :].bitcast(FP8X4),
+                    rhs_scale=ow_planes[:, BANKS * h + c, :],
+                    start=(h == 0 and c == 0),
+                    stop=(h == HEADS - 1 and c == BANKS - 1),
+                )
 
         def finish(u, parts=1):
             if not exists(u) or u % HEADS != HEADS - 1:
@@ -444,103 +409,97 @@ def tile_glamemoryreader_pb_k_kernel(
                 nc.vector.tensor_tensor(out=o_sb[:, cols], in0=accs[i][:, cols], in1=gate_sb[:, i, cols], op=ALU.mult)
                 nc.sync.dma_start(out=out_tiles[i][:, cols], in_=o_sb[:, cols])
 
-        def scalar_passes(u):
-            return 4 if u >= UNITS - 4 else 0 if u < 2 else 3
-
-        def normalise_pass(u, c, engine):
-            if c == 0:
-                rn = work.tile([P, HEAD_V], BF16, tag="rn")
-                normed[u] = rn
-            cols = slice(BANK * c, BANK * (c + 1))
-            if engine == "vector":
-                nc.vector.tensor_scalar(
-                    out=normed[u][:, cols], in0=weighed[u][:, cols], scalar1=rstds[u][:, 0:1], scalar2=1.0, op0=ALU.mult, op1=ALU.mult
-                )
-            else:
-                nc.scalar.activation(
-                    out=normed[u][:, cols], in_=weighed[u][:, cols], func=ACT.Copy, scale=rstds[u][:, 0:1]
-                )
-
-        def transpose_half(u, m, tag, bufs):
-            words = normed[u][:].bitcast(F32)
-            rt = psum.tile([P, 4, P], F32, tag=tag, bufs=bufs)
-            for j in range(4):
-                nc.tensor.transpose(
-                    out=rt[:, j, :], in_=words[:, P * (4 * m + j) : P * (4 * m + j + 1)], identity=ident_f32[:]
-                )
-            turned[(u, m)] = rt
-
-        def quantise_half(u, m):
-            if m == 0:
-                code = work.tile([P, BANKS, P], U32, tag="code", align_bytes=64)
-                plane = work.tile([P, BANKS, P], U8, tag="plane", align_bytes=64)
-                codes[u] = code
-                planes[u] = plane
-            two = slice(2 * m, 2 * m + 2)
-            nc.vector.quantize_mx(
-                out=codes[u][:, two, :].rearrange("p c t -> p (c t)").bitcast(FP8X4),
-                scales=planes[u][:, two, :].rearrange("p c t -> p (c t)"),
-                in_=groups[u][:, two, :, :].rearrange("p c t w -> p (c t w)"),
+        warm = keep.tile([P, 2], F32)
+        nc.scalar.activation(out=warm[:, 0:1], in_=eps_sb[:], func=ACT.Abs_reciprocal_sqrt)
+        for b in range(BATCH):
+            x_root(b)
+        for m in range(BANKS // 2):
+            nc.scalar.copy(
+                out=w_sorted[:, 2 * BANK * m : 2 * BANK * (m + 1)], in_=v_norm_ps[m][:].rearrange("p j k -> p (j k)")
             )
+        turn_queries(0)
+        keep_queries(0, nc.scalar.copy)
+        for b in range(BATCH):
+            x_normalise(b)
+            x_turn(b)
+            if b < 2:
+                x_regroup(b, nc.scalar.copy)
+        nc.scalar.activation(out=warm[:, 1:2], in_=eps_sb[:], func=ACT.Sigmoid)
+        x_quantise(0)
+        x_quantise(1)
+        for b in range(2, BATCH):
+            x_regroup(b, nc.vector.tensor_copy)
+            x_quantise(b)
 
         for u in range(-1, UNITS):
             finish(u - 5)
-            gate(2 * u + 2)
-            gate(2 * u + 3)
+            for i in range(2 * u + 2, 2 * u + 4):
+                multiply_gate(i)
             for c in range(BANKS // 2):
                 square(u, c + 2)
                 weigh(u, c)
                 read(u + 1, c)
-                project(u - 4, 2 * c)
-                project(u - 4, 2 * c + 1)
+                project(u - 4, 2 * c, 2 * c + 2)
             turn_queries(u + 2)
-            partial(u)
-            if u == UNITS - 1:
-                for c in range(BANKS):
-                    project(u - 3, c)
-            gate_out(2 * u + 2)
-            gate_out(2 * u + 3)
-            regroup(u - 2, nc.scalar.copy, 0, min(scalar_passes(u - 2), 2) - 1)
+            if u >= POW_UNITS:
+                add_squares(u, BANKS - 1)
+            if u == LAST:
+                project(u - 3)
+            for i in range(2 * u + 2, 2 * u + 4):
+                open_gate(i)
+            on_scalar = scalar_passes(u - 2)
+            regroup(u - 2, nc.scalar.copy, 0, min(on_scalar, 2))
             weigh(u, 2)
             read(u + 1, 2)
-            root(u)
-            regroup(u - 2, nc.scalar.copy, 2, scalar_passes(u - 2) - 1)
+            if u >= POW_UNITS:
+                root(u)
+            regroup(u - 2, nc.scalar.copy, 2, on_scalar)
             weigh(u, 3)
             read(u + 1, 3)
+            if u < POW_UNITS:
+                add_squares(u, BANKS)
+                root_by_pow(u)
             keep_queries(u + 2, nc.vector.tensor_copy)
             square(u + 1, 0)
             square(u + 1, 1)
-            if u < UNITS - 1:
+            if u < LAST:
                 normalise(u)
                 quantise(u - 3)
-            if u >= UNITS - 2:
+            if u >= LAST - 1:
                 quantise(u - 2)
-            if scalar_passes(u - 2) == 0:
-                regroup(u - 2, nc.vector.tensor_copy, 0, 1)
-            regroup(u - 2, nc.vector.tensor_copy, max(scalar_passes(u - 2), 2), BANKS - 1)
-            transpose(u - 1)
+            regroup(u - 2, nc.vector.tensor_copy, on_scalar, 2)
+            regroup(u - 2, nc.vector.tensor_copy, max(on_scalar, 2), BANKS)
+            transpose(u - 1, "turn", 2)
             if HEADS <= u < 2 * HEADS:
                 load_state(STATE_BUFS + u - HEADS)
-        last = UNITS - 1
-        sc, ve = nc.scalar.copy, nc.vector.tensor_copy
-        normalise_pass(last, 0, "scalar")
-        normalise_pass(last, 1, "scalar")
-        normalise_pass(last, 2, "vector")
-        normalise_pass(last, 3, "vector")
-        regroup(last - 1, sc, 0, 1)
-        regroup(last - 1, ve, 2, 3)
-        quantise(last - 1)
-        transpose_half(last, 0, "read", READ_BANKS)
-        transpose_half(last, 1, "read", READ_BANKS)
+
+        rn_last = work.tile([P, HEAD_V], BF16, tag="rn")
+        normed[LAST] = rn_last
         for c in range(BANKS):
-            project(last - 2, c)
-        regroup(last, sc, 0, 1)
-        regroup(last, ve, 2, 3)
-        for c in range(BANKS):
-            project(last - 1, c)
-        quantise_half(last, 0)
-        quantise_half(last, 1)
-        finish(last - 4)
-        for c in range(BANKS):
-            project(last, c)
-        finish(last, 2)
+            cols = slice(BANK * c, BANK * (c + 1))
+            if c < 2:
+                nc.scalar.activation(
+                    out=rn_last[:, cols], in_=weighed[LAST][:, cols], func=ACT.Copy, scale=rstds[LAST][:, 0:1]
+                )
+            else:
+                nc.vector.tensor_scalar(
+                    out=rn_last[:, cols],
+                    in0=weighed[LAST][:, cols],
+                    scalar1=rstds[LAST][:, 0:1],
+                    scalar2=1.0,
+                    op0=ALU.mult,
+                    op1=ALU.mult,
+                )
+        regroup(LAST - 1, nc.scalar.copy, 0, 2)
+        regroup(LAST - 1, nc.vector.tensor_copy, 2, 4)
+        quantise(LAST - 1)
+        transpose(LAST, "read", READ_BANKS)
+        project(LAST - 2)
+        regroup(LAST, nc.scalar.copy, 0, 2)
+        regroup(LAST, nc.vector.tensor_copy, 2, 4)
+        project(LAST - 1)
+        quantise(LAST, 0, 2)
+        quantise(LAST, 2, 4)
+        finish(LAST - 4)
+        project(LAST)
+        finish(LAST, 2)

@@ -25,6 +25,7 @@ BANK = 512
 BANKS = HEAD_V // BANK
 UNITS = TOKEN_TILES * HEADS
 LAST = UNITS - 1
+SHARED = LAST - 3
 STATE_BUFS = 12
 READ_BANKS = 4
 POW_UNITS = 3
@@ -271,6 +272,7 @@ def tile_glamemoryreader_pb_k_kernel(
         codes = {}
         planes = {}
         accs = {}
+        half_accs = {}
 
         def exists(u):
             return 0 <= u < UNITS
@@ -355,30 +357,36 @@ def tile_glamemoryreader_pb_k_kernel(
                     )
                 turned[(u, m)] = rt
 
+        def place(u, c):
+            if u > SHARED:
+                return ("own", u), c
+            return ("shared", u + c // 2), (c + 2) % BANKS
+
         def regroup(u, copy, first, end):
             if not exists(u) or first >= end:
                 return
-            if first == 0:
+            group, j = place(u, first)
+            if group not in groups:
                 grouped = work.tile([P, BANKS, P, 4], BF16, tag="grouped", align_bytes=64)
-                groups[u] = grouped
+                groups[group] = grouped
             m = first // 2
             copy(
-                out=groups[u][:, first:end, :, :].bitcast(F32),
+                out=groups[group][:, j : j + end - first, :, :].bitcast(F32),
                 in_=turned[(u, m)][:, 2 * first - 4 * m : 2 * end - 4 * m, :].rearrange("p (c s) t -> p c t s", s=2),
             )
 
-        def quantise(u, first=0, end=BANKS):
-            if not exists(u):
+        def quantise(group, first=0, end=BANKS):
+            if group not in groups:
                 return
-            if first == 0:
+            if group not in codes:
                 code = work.tile([P, BANKS, P], U32, tag="code", align_bytes=64)
                 plane = work.tile([P, BANKS, P], U8, tag="plane", align_bytes=64)
-                codes[u] = code
-                planes[u] = plane
+                codes[group] = code
+                planes[group] = plane
             nc.vector.quantize_mx(
-                out=codes[u][:, first:end, :].rearrange("p c t -> p (c t)").bitcast(FP8X4),
-                scales=planes[u][:, first:end, :].rearrange("p c t -> p (c t)"),
-                in_=groups[u][:, first:end, :, :].rearrange("p c t w -> p (c t w)"),
+                out=codes[group][:, first:end, :].rearrange("p c t -> p (c t)").bitcast(FP8X4),
+                scales=planes[group][:, first:end, :].rearrange("p c t -> p (c t)"),
+                in_=groups[group][:, first:end, :, :].rearrange("p c t w -> p (c t w)"),
             )
 
         def project(u, first=0, end=BANKS):
@@ -386,18 +394,45 @@ def tile_glamemoryreader_pb_k_kernel(
                 return
             h = u % HEADS
             for c in range(first, end):
+                group, j = place(u, c)
                 if h == 0 and c == 0:
                     acc = psum.tile([P, D_MODEL], F32, tag="acc", bufs=2)
                     accs[u // HEADS] = acc
                 nc.tensor.matmul_mx(
                     out=accs[u // HEADS][:],
-                    lhsT=codes[u][:, c, :].bitcast(FP8X4),
-                    lhsT_scale=planes[u][:, c, :],
+                    lhsT=codes[group][:, j, :].bitcast(FP8X4),
+                    lhsT_scale=planes[group][:, j, :],
                     rhs=ow_words[h][:, c, :].bitcast(FP8X4),
                     rhs_scale=ow_planes[:, BANKS * h + c, :],
                     start=(h == 0 and c == 0),
                     stop=(h == HEADS - 1 and c == BANKS - 1),
                 )
+
+        def project_half(u, half, first=0, end=BANKS):
+            h = u % HEADS
+            cols = slice(D_MODEL // 2 * half, D_MODEL // 2 * (half + 1))
+            for c in range(first, end):
+                group, j = place(u, c)
+                if h == 0 and c == 0:
+                    half_acc = psum.tile([P, D_MODEL // 2], F32, tag="acc" if half == 0 else "read", bufs=2 if half == 0 else READ_BANKS)
+                    half_accs[half] = half_acc
+                nc.tensor.matmul_mx(
+                    out=half_accs[half][:],
+                    lhsT=codes[group][:, j, :].bitcast(FP8X4),
+                    lhsT_scale=planes[group][:, j, :],
+                    rhs=ow_words[h][:, c, cols].bitcast(FP8X4),
+                    rhs_scale=ow_planes[:, BANKS * h + c, cols],
+                    start=(h == 0 and c == 0),
+                    stop=(h == HEADS - 1 and c == BANKS - 1),
+                )
+
+        def finish_half(half):
+            cols = slice(D_MODEL // 2 * half, D_MODEL // 2 * (half + 1))
+            o_half = work.tile([P, D_MODEL // 2], F32, tag="o_half", bufs=2)
+            nc.vector.tensor_tensor(
+                out=o_half[:], in0=half_accs[half][:], in1=gate_sb[:, TOKEN_TILES - 1, cols], op=ALU.mult
+            )
+            nc.sync.dma_start(out=out_tiles[TOKEN_TILES - 1][:, cols], in_=o_half[:])
 
         def finish(u, parts=1):
             if not exists(u) or u % HEADS != HEADS - 1:
@@ -439,15 +474,19 @@ def tile_glamemoryreader_pb_k_kernel(
                 square(u, c + 2)
                 weigh(u, c)
                 read(u + 1, c)
-                project(u - 4, 2 * c, 2 * c + 2)
+                if u == LAST and c == 1:
+                    continue
+                project(u - 4 + c, 2 - 2 * c, 4 - 2 * c)
             turn_queries(u + 2)
             if u >= POW_UNITS:
                 add_squares(u, BANKS - 1)
             if u == LAST:
-                project(u - 3)
+                for half in range(2):
+                    project_half(u - 3, half)
             for i in range(2 * u + 2, 2 * u + 4):
                 open_gate(i)
             on_scalar = scalar_passes(u - 2)
+            regroup(u - 2, nc.vector.tensor_copy, on_scalar, 2)
             regroup(u - 2, nc.scalar.copy, 0, min(on_scalar, 2))
             weigh(u, 2)
             read(u + 1, 2)
@@ -464,10 +503,14 @@ def tile_glamemoryreader_pb_k_kernel(
             square(u + 1, 1)
             if u < LAST:
                 normalise(u)
-                quantise(u - 3)
-            if u >= LAST - 1:
-                quantise(u - 2)
-            regroup(u - 2, nc.vector.tensor_copy, on_scalar, 2)
+                if u > 2:
+                    quantise(("shared", u - 2))
+                elif u == 2:
+                    quantise(("shared", 0), 2, 4)
+            if u == LAST - 1:
+                quantise(("shared", u - 1), 0, 2)
+            if u == LAST:
+                quantise(("own", u - 2))
             regroup(u - 2, nc.vector.tensor_copy, max(on_scalar, 2), BANKS)
             transpose(u - 1, "turn", 2)
             if HEADS <= u < 2 * HEADS:
@@ -492,14 +535,17 @@ def tile_glamemoryreader_pb_k_kernel(
                 )
         regroup(LAST - 1, nc.scalar.copy, 0, 2)
         regroup(LAST - 1, nc.vector.tensor_copy, 2, 4)
-        quantise(LAST - 1)
+        quantise(("own", LAST - 1))
         transpose(LAST, "read", READ_BANKS)
-        project(LAST - 2)
+        for half in range(2):
+            project_half(LAST - 2, half)
         regroup(LAST, nc.scalar.copy, 0, 2)
         regroup(LAST, nc.vector.tensor_copy, 2, 4)
-        project(LAST - 1)
-        quantise(LAST, 0, 2)
-        quantise(LAST, 2, 4)
+        for half in range(2):
+            project_half(LAST - 1, half)
+        quantise(("own", LAST), 0, 2)
+        quantise(("own", LAST), 2, 4)
         finish(LAST - 4)
-        project(LAST)
-        finish(LAST, 2)
+        for half in range(2):
+            project_half(LAST, half)
+            finish_half(half)

@@ -36,7 +36,7 @@ FLOPS = 2 * (1024 * 8192 * 512 + 1024 * 512 * 512 + 16 * 256 * 128 * 2048)
 def scalar_passes(u):
     if u < 2:
         return 0
-    return 3 if u < UNITS - 4 else 4
+    return 4 if u % HEADS == 1 or u >= UNITS - 4 else 3
 
 
 def tile_glamemoryreader_pb_k_kernel(
@@ -110,8 +110,9 @@ def tile_glamemoryreader_pb_k_kernel(
             states[bh] = state
 
         load_x(0)
+        load_x(1)
         nc.sync.dma_start(out=norm_row[0:1, :], in_=norm_w.unsqueeze(0))
-        for b in range(1, BATCH):
+        for b in range(2, BATCH):
             load_x(b)
         nc.sync.dma_start(out=v_norm_row[0:1, :], in_=v_norm_w.unsqueeze(0))
         nc.sync.dma_start(out=q_sb[:, pair(0), :], in_=q_dram[:, pair(0), :])
@@ -230,6 +231,11 @@ def tile_glamemoryreader_pb_k_kernel(
                         identity=ident_f32[:],
                     )
             x_turned[b] = xt
+
+        def keep_clock(n):
+            unread = psum.tile([P, BANK], F32, tag="read", bufs=READ_BANKS)
+            for m in range(n):
+                nc.tensor.matmul(out=unread[:], lhsT=ones[:], rhs=v_norm_row[:, 0:BANK], start=True, stop=True)
 
         def x_regroup(b, copy):
             xg = keep.tile([P, TILES_PER_BATCH, P, 4], BF16, tag="xg", bufs=2, align_bytes=64)
@@ -457,6 +463,8 @@ def tile_glamemoryreader_pb_k_kernel(
         for b in range(BATCH):
             x_normalise(b)
             x_turn(b)
+            if b in (0, 2,):
+                keep_clock(2)
             if b < 2:
                 x_regroup(b, nc.scalar.copy)
         nc.scalar.activation(out=warm[:, 1:2], in_=eps_sb[:], func=ACT.Sigmoid)

@@ -518,7 +518,8 @@ def tile_glamemoryreader_pb_k_kernel(
             if u == LAST - 1:
                 quantise(("shared", u - 1), 0, 2)
             if u == LAST:
-                quantise(("own", u - 2))
+                quantise(("own", u - 2), 0, 2)
+                quantise(("own", u - 2), 2, 4)
             regroup(u - 2, nc.vector.tensor_copy, max(on_scalar, 2), BANKS)
             transpose(u - 1, "turn", 2)
             if HEADS <= u < 2 * HEADS:
@@ -544,9 +545,9 @@ def tile_glamemoryreader_pb_k_kernel(
         regroup(LAST - 1, nc.scalar.copy, 0, 2)
         regroup(LAST - 1, nc.vector.tensor_copy, 2, 4)
         quantise(("own", LAST - 1))
+        project_half(LAST - 2, 0)
         transpose(LAST, "read", READ_BANKS)
-        for half in range(2):
-            project_half(LAST - 2, half)
+        project_half(LAST - 2, 1)
         regroup(LAST, nc.scalar.copy, 0, 2)
         regroup(LAST, nc.vector.tensor_copy, 2, 4)
         for half in range(2):

@@ -59,10 +59,9 @@ def tile_glamemoryreader_pb_k_kernel(
         psum = ctx.enter_context(tc.psum_pool(name="psum", bufs=1))
         ctx.enter_context(tc.manual_schedule())
 
-        ident_bf16 = keep.tile([P, P], BF16)
-        make_identity(nc, ident_bf16[:])
         ident_f32 = keep.tile([P, P], F32)
         make_identity(nc, ident_f32[:])
+        ident_bf16 = keep.tile([P, P], BF16)
         norm_row = keep.tile([P, D_MODEL], BF16)
         nc.vector.memset(norm_row[:].bitcast(I32), 0)
         v_norm_row = keep.tile([P, HEAD_V], BF16)
@@ -180,8 +179,11 @@ def tile_glamemoryreader_pb_k_kernel(
         x_grouped = {}
         gate_ps = {}
 
-        def x_root(b):
+        x_mean_squares = {}
+
+        def x_squares(b):
             x_ms = keep.tile([P, TILES_PER_BATCH], F32, tag="x_ms", bufs=BATCH)
+            x_mean_squares[b] = x_ms
             for j in range(TILES_PER_BATCH):
                 x_sq = keep.tile([P, D_MODEL], BF16, tag="x_sq_%d" % j, bufs=2)
                 x_tile = x_sb[:, TILES_PER_BATCH * b + j, :]
@@ -203,8 +205,10 @@ def tile_glamemoryreader_pb_k_kernel(
                         op1=ALU.mult,
                         accum_out=x_ms[:, j : j + 1],
                     )
+
+        def x_root(b):
             nc.scalar.activation(
-                out=x_rstd[:, pair(b)], in_=x_ms[:], func=ACT.Abs_reciprocal_sqrt, bias=eps_sb[:, 0:1]
+                out=x_rstd[:, pair(b)], in_=x_mean_squares[b][:], func=ACT.Abs_reciprocal_sqrt, bias=eps_sb[:, 0:1]
             )
 
         def x_normalise(b):
@@ -453,6 +457,9 @@ def tile_glamemoryreader_pb_k_kernel(
         warm = keep.tile([P, 2], F32)
         nc.scalar.activation(out=warm[:, 0:1], in_=eps_sb[:], func=ACT.Abs_reciprocal_sqrt)
         for b in range(BATCH):
+            x_squares(b)
+            if b == 0:
+                nc.scalar.copy(out=ident_bf16[:], in_=ident_f32[:])
             x_root(b)
         for m in range(BANKS // 2):
             nc.scalar.copy(
@@ -472,6 +479,7 @@ def tile_glamemoryreader_pb_k_kernel(
         x_quantise(1)
         for b in range(2, BATCH):
             x_regroup(b, nc.vector.tensor_copy)
+        for b in range(2, BATCH):
             x_quantise(b)
 
         for u in range(-1, UNITS):

from contextlib import ExitStack

import concourse.mybir as mybir
from concourse.masks import make_identity

F32 = mybir.dt.float32
BF16 = mybir.dt.bfloat16
I32 = mybir.dt.int32
U32 = mybir.dt.uint32
U8 = mybir.dt.uint8
FP8X4 = mybir.dt.float8_e4m3fn_x4
ACT = mybir.ActivationFunctionType
ALU = mybir.AluOpType
AXIS = mybir.AxisListType

P = 128
BATCH = 4
SEQ = 256
D_MODEL = 512
HEADS = 4
HEAD_V = 2048
TILES_PER_BATCH = SEQ // P
TOKEN_TILES = BATCH * TILES_PER_BATCH
BANK = 512
BANKS = HEAD_V // BANK
UNITS = TOKEN_TILES * HEADS
LAST = UNITS - 1
SHARED = LAST - 3
STATE_BUFS = 12
READ_BANKS = 4
POW_UNITS = 3
EPS = 1e-5
FLOPS = 2 * (1024 * 8192 * 512 + 1024 * 512 * 512 + 16 * 256 * 128 * 2048)


def scalar_passes(u):
    if u < 2:
        return 0
    return 4 if u % HEADS == 1 or u >= UNITS - 4 else 3


def tile_glamemoryreader_pb_k_kernel(
    tc,
    hidden_states,
    norm_w,
    gate_w_words,
    gate_w_scales,
    q_hat,
    recurrent_state,
    v_norm_w,
    o_w_words,
    o_w_scales,
    out,
):
    nc = tc.nc
    with ExitStack() as ctx:
        keep = ctx.enter_context(tc.tile_pool(name="keep", bufs=1))
        work = ctx.enter_context(tc.tile_pool(name="work", bufs=3))
        psum = ctx.enter_context(tc.psum_pool(name="psum", bufs=1))
        ctx.enter_context(tc.manual_schedule())

        ident_f32 = keep.tile([P, P], F32)
        make_identity(nc, ident_f32[:])
        ident_bf16 = keep.tile([P, P], BF16)
        norm_row = keep.tile([P, D_MODEL], BF16)
        nc.vector.memset(norm_row[:].bitcast(I32), 0)
        v_norm_row = keep.tile([P, HEAD_V], BF16)
        nc.vector.memset(v_norm_row[:].bitcast(I32), 0)
        ones = keep.tile([P, P], BF16)
        nc.vector.memset(ones[:], 1.0)
        eps_sb = keep.tile([P, 1], F32)
        nc.vector.memset(eps_sb[:], EPS)
        minus_half = keep.tile([P, 1], F32)
        nc.vector.memset(minus_half[:], -0.5)
        gw_planes = keep.tile([P, D_MODEL], U8, align_bytes=64)
        nc.vector.memset(gw_planes[:].bitcast(I32), 0)
        ow_planes = keep.tile([P, HEADS * BANKS, D_MODEL], U8, align_bytes=64)
        nc.vector.memset(ow_planes[:].bitcast(I32), 0)
        sums = keep.tile([P, UNITS, 8], F32)
        nc.vector.memset(sums[:], EPS)

        gate_sb = keep.tile([P, TOKEN_TILES, D_MODEL], F32)
        q_t = keep.tile([P, UNITS, P], BF16)
        w_sorted = keep.tile([P, HEAD_V], BF16)
        x_sb = keep.tile([P, TOKEN_TILES, D_MODEL], BF16)
        q_sb = keep.tile([P, TOKEN_TILES, HEADS * P], BF16)
        gw_words = keep.tile([P, D_MODEL], U32, align_bytes=64)
        ow_words = [
            keep.tile([P, BANKS, D_MODEL], U32, name="ow_words_%d" % h, align_bytes=64) for h in range(HEADS)
        ]
        x_rstd = keep.tile([P, TOKEN_TILES], F32)
        x_codes = keep.tile([P, TOKEN_TILES, P], U32, align_bytes=64)
        x_planes = keep.tile([P, TOKEN_TILES, P], U8, align_bytes=64)

        x_dram = hidden_states.rearrange("b (i p) d -> p (b i) d", p=P)
        q_dram = q_hat.rearrange("b (i p) h k -> p (b i) (h k)", p=P)
        out_tiles = out.rearrange("b (i p) d -> (b i) p d", p=P)
        states = {}

        def pair(b):
            return slice(TILES_PER_BATCH * b, TILES_PER_BATCH * (b + 1))

        def load_x(b):
            nc.sync.dma_start(out=x_sb[:, pair(b), :], in_=x_dram[:, pair(b), :])

        def load_state(bh):
            state = keep.tile([P, HEAD_V], BF16, tag="state", bufs=STATE_BUFS)
            nc.sync.dma_start(out=state[:], in_=recurrent_state[bh // HEADS, bh % HEADS])
            states[bh] = state

        load_x(0)
        load_x(1)
        nc.sync.dma_start(out=norm_row[0:1, :], in_=norm_w.unsqueeze(0))
        for b in range(2, BATCH):
            load_x(b)
        nc.sync.dma_start(out=v_norm_row[0:1, :], in_=v_norm_w.unsqueeze(0))
        nc.sync.dma_start(out=q_sb[:, pair(0), :], in_=q_dram[:, pair(0), :])
        load_state(0)
        nc.sync.dma_start(
            out=gw_words[:].bitcast(I32), in_=gate_w_words[0].rearrange("p n t -> p (n t)").bitcast(I32)
        )
        for r in range(4):
            nc.sync.dma_start(out=gw_planes[r:P:32, :].bitcast(I32), in_=gate_w_scales[0, r:16:4, :].bitcast(I32))
        load_state(1)
        nc.sync.dma_start(out=q_sb[:, TILES_PER_BATCH:, :], in_=q_dram[:, TILES_PER_BATCH:, :])
        load_state(2)
        load_state(3)
        for r in range(4):
            nc.sync.dma_start(
                out=ow_planes[r:P:32, :, :].bitcast(I32),
                in_=o_w_scales[:, r:16:4, :].rearrange("g c n -> c g n").bitcast(I32),
            )
        for h in range(HEADS):
            nc.sync.dma_start(
                out=ow_words[h][:].bitcast(I32),
                in_=o_w_words[BANKS * h : BANKS * (h + 1)].rearrange("g p n t -> p g (n t)").bitcast(I32),
            )
        for bh in range(HEADS, STATE_BUFS):
            load_state(bh)

        norm_ps = psum.tile([P, D_MODEL], F32, tag="acc", bufs=2)
        nc.tensor.matmul(out=norm_ps[:], lhsT=ones[:], rhs=norm_row[:], start=True, stop=True)
        v_norm_ps = []
        for m in range(BANKS // 2):
            two_passes = psum.tile([P, 2, BANK], BF16, tag="read", bufs=READ_BANKS)
            for j in range(2):
                c = 2 * m + j
                nc.tensor.matmul(
                    out=two_passes[:, j, :].rearrange("t (s p e) -> t p s e", s=2, e=2),
                    lhsT=ones[:],
                    rhs=v_norm_row[:, BANK * c : BANK * (c + 1)].rearrange("k (p s e) -> k p s e", s=2, e=2),
                    start=True,
                    stop=True,
                )
            v_norm_ps.append(two_passes)

        q_turned = {}

        def turn_queries(b):
            if b >= BATCH:
                return
            qt_ps = psum.tile([P, TILES_PER_BATCH * HEADS, P], BF16, tag="turn", bufs=2)
            for j in range(TILES_PER_BATCH * HEADS):
                h = j % HEADS
                nc.tensor.transpose(
                    out=qt_ps[:, j, :],
                    in_=q_sb[:, TILES_PER_BATCH * b + j // HEADS, P * h : P * (h + 1)],
                    identity=ident_bf16[:],
                )
            q_turned[b] = qt_ps

        def keep_queries(b, copy):
            if b < BATCH:
                units = slice(TILES_PER_BATCH * HEADS * b, TILES_PER_BATCH * HEADS * (b + 1))
                copy(out=q_t[:, units, :], in_=q_turned[b][:])

        x_normed = {}
        x_turned = {}
        x_grouped = {}
        gate_ps = {}

        x_mean_squares = {}

        def x_squares(b):
            x_ms = keep.tile([P, TILES_PER_BATCH], F32, tag="x_ms", bufs=BATCH)
            x_mean_squares[b] = x_ms
            for j in range(TILES_PER_BATCH):
                x_sq = keep.tile([P, D_MODEL], BF16, tag="x_sq_%d" % j, bufs=2)
                x_tile = x_sb[:, TILES_PER_BATCH * b + j, :]
                if j == 0:
                    nc.scalar.activation(
                        out=x_sq[:],
                        in_=x_tile,
                        func=ACT.Square,
                        scale=D_MODEL**-0.5,
                        accum_out=x_ms[:, j : j + 1],
                    )
                else:
                    nc.vector.scalar_tensor_tensor(
                        out=x_sq[:],
                        in0=x_tile,
                        scalar=1.0 / D_MODEL,
                        in1=x_tile,
                        op0=ALU.mult,
                        op1=ALU.mult,
                        accum_out=x_ms[:, j : j + 1],
                    )

        def x_root(b):
            nc.scalar.activation(
                out=x_rstd[:, pair(b)], in_=x_mean_squares[b][:], func=ACT.Abs_reciprocal_sqrt, bias=eps_sb[:, 0:1]
            )

        def x_normalise(b):
            xn = keep.tile([P, TILES_PER_BATCH, D_MODEL], BF16, tag="xn", bufs=2)
            for j in range(TILES_PER_BATCH):
                i = TILES_PER_BATCH * b + j
                nc.vector.scalar_tensor_tensor(
                    out=xn[:, j, :],
                    in0=x_sb[:, i, :],
                    scalar=x_rstd[:, i : i + 1],
                    in1=norm_ps[:],
                    op0=ALU.mult,
                    op1=ALU.mult,
                )
            x_normed[b] = xn

        def x_turn(b):
            xt = psum.tile([P, 2 * TILES_PER_BATCH, P], F32, tag="turn", bufs=2)
            for j in range(TILES_PER_BATCH):
                for s in range(2):
                    nc.tensor.transpose(
                        out=xt[:, 2 * j + s, :],
                        in_=x_normed[b][:, j, :].bitcast(F32)[:, s : D_MODEL // 2 : 2],
                        identity=ident_f32[:],
                    )
            x_turned[b] = xt

        def keep_clock(n):
            unread = psum.tile([P, BANK], F32, tag="read", bufs=READ_BANKS)
            for m in range(n):
                nc.tensor.matmul(out=unread[:], lhsT=ones[:], rhs=v_norm_row[:, 0:BANK], start=True, stop=True)

        def x_regroup(b, copy):
            xg = keep.tile([P, TILES_PER_BATCH, P, 4], BF16, tag="xg", bufs=2, align_bytes=64)
            copy(out=xg[:].bitcast(F32), in_=x_turned[b][:].rearrange("p (i s) t -> p i t s", s=2))
            x_grouped[b] = xg

        def x_quantise(b):
            nc.vector.quantize_mx(
                out=x_codes[:, pair(b), :].rearrange("p i t -> p (i t)").bitcast(FP8X4),
                scales=x_planes[:, pair(b), :].rearrange("p i t -> p (i t)"),
                in_=x_grouped[b][:].rearrange("p i t w -> p (i t w)"),
            )

        def multiply_gate(i):
            if i >= TOKEN_TILES:
                return
            product = psum.tile([P, D_MODEL], F32, tag="acc", bufs=2)
            nc.tensor.matmul_mx(
                out=product[:],
                lhsT=x_codes[:, i, :].bitcast(FP8X4),
                lhsT_scale=x_planes[:, i, :],
                rhs=gw_words[:].bitcast(FP8X4),
                rhs_scale=gw_planes[:],
                start=True,
                stop=True,
            )
            gate_ps[i] = product

        def open_gate(i):
            if i < TOKEN_TILES:
                nc.scalar.activation(out=gate_sb[:, i, :], in_=gate_ps[i][:], func=ACT.Sigmoid)

        r_banks = {}
        partial_sums = {}
        rstds = {}
        weighed = {}
        normed = {}
        turned = {}
        groups = {}
        codes = {}
        planes = {}
        accs = {}
        half_accs = {}

        def exists(u):
            return 0 <= u < UNITS

        def read(u, c):
            if not exists(u):
                return
            r_bank = psum.tile([P, BANK], F32, tag="read", bufs=READ_BANKS)
            bh = HEADS * (u // HEADS // TILES_PER_BATCH) + u % HEADS
            nc.tensor.matmul(
                out=r_bank[:].rearrange("t (s p e) -> t p s e", s=2, e=2),
                lhsT=q_t[:, u, :],
                rhs=states[bh][:, BANK * c : BANK * (c + 1)].rearrange("k (p s e) -> k p s e", s=2, e=2),
                start=True,
                stop=True,
            )
            r_banks[(u, c)] = r_bank

        def square(u, c):
            if not exists(u):
                return
            sq = work.tile([P, BANK], BF16, tag="sq", bufs=4)
            nc.scalar.activation(
                out=sq[:],
                in_=r_banks[(u, c)][:],
                func=ACT.Square,
                scale=HEAD_V**-0.5,
                accum_out=sums[:, u, c + 1 : c + 2],
            )

        def weigh(u, c):
            if not exists(u):
                return
            if c == 0:
                y = work.tile([P, HEAD_V], F32, tag="y")
                weighed[u] = y
            cols = slice(BANK * c, BANK * (c + 1))
            nc.vector.tensor_tensor(out=weighed[u][:, cols], in0=r_banks[(u, c)][:], in1=w_sorted[:, cols], op=ALU.mult)

        def add_squares(u, banks):
            if not exists(u):
                return
            partial = work.tile([P, 1], F32, tag="partial", bufs=4)
            nc.vector.tensor_reduce(out=partial[:], in_=sums[:, u, 0 : banks + 1], axis=AXIS.X, op=ALU.add)
            partial_sums[u] = partial

        def root_by_pow(u):
            if not exists(u):
                return
            rstd = work.tile([P, 1], F32, tag="rstd", bufs=4)
            nc.gpsimd.tensor_tensor(out=rstd[:], in0=partial_sums[u][:], in1=minus_half[:], op=ALU.pow)
            rstds[u] = rstd

        def root(u):
            rstd = work.tile([P, 1], F32, tag="rstd", bufs=4)
            nc.scalar.activation(
                out=rstd[:],
                in_=sums[:, u, BANKS : BANKS + 1],
                func=ACT.Abs_reciprocal_sqrt,
                bias=partial_sums[u][:, 0:1],
            )
            rstds[u] = rstd

        def normalise(u):
            if not exists(u):
                return
            rn = work.tile([P, HEAD_V], BF16, tag="rn")
            nc.gpsimd.tensor_scalar(
                out=rn[:], in0=weighed[u][:], scalar1=rstds[u][:, 0:1], scalar2=1.0, op0=ALU.mult, op1=ALU.mult
            )
            normed[u] = rn

        def transpose(u, tag, bufs):
            if not exists(u):
                return
            words = normed[u][:].bitcast(F32)
            for m in range(BANKS // 2):
                rt = psum.tile([P, 4, P], F32, tag=tag, bufs=bufs)
                for j in range(4):
                    nc.tensor.transpose(
                        out=rt[:, j, :], in_=words[:, P * (4 * m + j) : P * (4 * m + j + 1)], identity=ident_f32[:]
                    )
                turned[(u, m)] = rt

        def place(u, c):
            if u > SHARED:
                return ("own", u), c
            return ("shared", u + c // 2), (c + 2) % BANKS

        def regroup(u, copy, first, end):
            if not exists(u) or first >= end:
                return
            group, j = place(u, first)
            if group not in groups:
                grouped = work.tile([P, BANKS, P, 4], BF16, tag="grouped", align_bytes=64)
                groups[group] = grouped
            m = first // 2
            copy(
                out=groups[group][:, j : j + end - first, :, :].bitcast(F32),
                in_=turned[(u, m)][:, 2 * first - 4 * m : 2 * end - 4 * m, :].rearrange("p (c s) t -> p c t s", s=2),
            )

        def quantise(group, first=0, end=BANKS):
            if group not in groups:
                return
            if group not in codes:
                code = work.tile([P, BANKS, P], U32, tag="code", align_bytes=64)
                plane = work.tile([P, BANKS, P], U8, tag="plane", align_bytes=64)
                codes[group] = code
                planes[group] = plane
            nc.vector.quantize_mx(
                out=codes[group][:, first:end, :].rearrange("p c t -> p (c t)").bitcast(FP8X4),
                scales=planes[group][:, first:end, :].rearrange("p c t -> p (c t)"),
                in_=groups[group][:, first:end, :, :].rearrange("p c t w -> p (c t w)"),
            )

        def project(u, first=0, end=BANKS):
            if not exists(u):
                return
            h = u % HEADS
            for c in range(first, end):
                group, j = place(u, c)
                if h == 0 and c == 0:
                    acc = psum.tile([P, D_MODEL], F32, tag="acc", bufs=2)
                    accs[u // HEADS] = acc
                nc.tensor.matmul_mx(
                    out=accs[u // HEADS][:],
                    lhsT=codes[group][:, j, :].bitcast(FP8X4),
                    lhsT_scale=planes[group][:, j, :],
                    rhs=ow_words[h][:, c, :].bitcast(FP8X4),
                    rhs_scale=ow_planes[:, BANKS * h + c, :],
                    start=(h == 0 and c == 0),
                    stop=(h == HEADS - 1 and c == BANKS - 1),
                )

        def project_half(u, half, first=0, end=BANKS):
            h = u % HEADS
            cols = slice(D_MODEL // 2 * half, D_MODEL // 2 * (half + 1))
            for c in range(first, end):
                group, j = place(u, c)
                if h == 0 and c == 0:
                    half_acc = psum.tile([P, D_MODEL // 2], F32, tag="acc" if half == 0 else "read", bufs=2 if half == 0 else READ_BANKS)
                    half_accs[half] = half_acc
                nc.tensor.matmul_mx(
                    out=half_accs[half][:],
                    lhsT=codes[group][:, j, :].bitcast(FP8X4),
                    lhsT_scale=planes[group][:, j, :],
                    rhs=ow_words[h][:, c, cols].bitcast(FP8X4),
                    rhs_scale=ow_planes[:, BANKS * h + c, cols],
                    start=(h == 0 and c == 0),
                    stop=(h == HEADS - 1 and c == BANKS - 1),
                )

        def finish_half(half):
            cols = slice(D_MODEL // 2 * half, D_MODEL // 2 * (half + 1))
            o_half = work.tile([P, D_MODEL // 2], F32, tag="o_half", bufs=2)
            nc.vector.tensor_tensor(
                out=o_half[:], in0=half_accs[half][:], in1=gate_sb[:, TOKEN_TILES - 1, cols], op=ALU.mult
            )
            nc.sync.dma_start(out=out_tiles[TOKEN_TILES - 1][:, cols], in_=o_half[:])

        def finish(u, parts=1):
            if not exists(u) or u % HEADS != HEADS - 1:
                return
            i = u // HEADS
            o_sb = work.tile([P, D_MODEL], F32, tag="o_sb", bufs=2)
            for part in range(parts):
                cols = slice(D_MODEL // parts * part, D_MODEL // parts * (part + 1))
                nc.vector.tensor_tensor(out=o_sb[:, cols], in0=accs[i][:, cols], in1=gate_sb[:, i, cols], op=ALU.mult)
                nc.sync.dma_start(out=out_tiles[i][:, cols], in_=o_sb[:, cols])

        warm = keep.tile([P, 2], F32)
        nc.scalar.activation(out=warm[:, 0:1], in_=eps_sb[:], func=ACT.Abs_reciprocal_sqrt)
        for b in range(BATCH):
            x_squares(b)
            if b == 0:
                nc.scalar.copy(out=ident_bf16[:], in_=ident_f32[:])
            x_root(b)
        for m in range(BANKS // 2):
            nc.scalar.copy(
                out=w_sorted[:, 2 * BANK * m : 2 * BANK * (m + 1)], in_=v_norm_ps[m][:].rearrange("p j k -> p (j k)")
            )
        turn_queries(0)
        keep_queries(0, nc.scalar.copy)
        for b in range(BATCH):
            x_normalise(b)
            x_turn(b)
            if b in (0, 2,):
                keep_clock(2)
            if b < 2:
                x_regroup(b, nc.scalar.copy)
        nc.scalar.activation(out=warm[:, 1:2], in_=eps_sb[:], func=ACT.Sigmoid)
        x_quantise(0)
        x_quantise(1)
        for b in range(2, BATCH):
            x_regroup(b, nc.vector.tensor_copy)
        for b in range(2, BATCH):
            x_quantise(b)

        for u in range(-1, UNITS):
            finish(u - 5)
            for i in range(2 * u + 2, 2 * u + 4):
                multiply_gate(i)
            for c in range(BANKS // 2):
                square(u, c + 2)
                weigh(u, c)
                read(u + 1, c)
                if u == LAST and c == 1:
                    continue
                project(u - 4 + c, 2 - 2 * c, 4 - 2 * c)
            turn_queries(u + 2)
            if u >= POW_UNITS:
                add_squares(u, BANKS - 1)
            if u == LAST:
                for half in range(2):
                    project_half(u - 3, half)
            for i in range(2 * u + 2, 2 * u + 4):
                open_gate(i)
            on_scalar = scalar_passes(u - 2)
            regroup(u - 2, nc.vector.tensor_copy, on_scalar, 2)
            regroup(u - 2, nc.scalar.copy, 0, min(on_scalar, 2))
            weigh(u, 2)
            read(u + 1, 2)
            if u >= POW_UNITS:
                root(u)
            regroup(u - 2, nc.scalar.copy, 2, on_scalar)
            weigh(u, 3)
            read(u + 1, 3)
            if u < POW_UNITS:
                add_squares(u, BANKS)
                root_by_pow(u)
            keep_queries(u + 2, nc.vector.tensor_copy)
            square(u + 1, 0)
            square(u + 1, 1)
            if u < LAST:
                normalise(u)
                if u > 2:
                    quantise(("shared", u - 2))
                elif u == 2:
                    quantise(("shared", 0), 2, 4)
            if u == LAST - 1:
                quantise(("shared", u - 1), 0, 2)
            if u == LAST:
                quantise(("own", u - 2), 0, 2)
                quantise(("own", u - 2), 2, 4)
            regroup(u - 2, nc.vector.tensor_copy, max(on_scalar, 2), BANKS)
            transpose(u - 1, "turn", 2)
            if HEADS <= u < 2 * HEADS:
                load_state(STATE_BUFS + u - HEADS)

        rn_last = work.tile([P, HEAD_V], BF16, tag="rn")
        normed[LAST] = rn_last
        for c in range(BANKS):
            cols = slice(BANK * c, BANK * (c + 1))
            if c < 2:
                nc.scalar.activation(
                    out=rn_last[:, cols], in_=weighed[LAST][:, cols], func=ACT.Copy, scale=rstds[LAST][:, 0:1]
                )
            else:
                nc.vector.tensor_scalar(
                    out=rn_last[:, cols],
                    in0=weighed[LAST][:, cols],
                    scalar1=rstds[LAST][:, 0:1],
                    scalar2=1.0,
                    op0=ALU.mult,
                    op1=ALU.mult,
                )
        regroup(LAST - 1, nc.scalar.copy, 0, 2)
        regroup(LAST - 1, nc.vector.tensor_copy, 2, 4)
        quantise(("own", LAST - 1))
        project_half(LAST - 2, 0)
        transpose(LAST, "read", READ_BANKS)
        project_half(LAST - 2, 1)
        regroup(LAST, nc.scalar.copy, 0, 2)
        regroup(LAST, nc.vector.tensor_copy, 2, 4)
        for half in range(2):
            project_half(LAST - 1, half)
        quantise(("own", LAST), 0, 2)
        quantise(("own", LAST), 2, 4)
        finish(LAST - 4)
        for half in range(2):
            project_half(LAST, half)
            finish_half(half)
